import numpy as np
import ml_dtypes


def mxq(x, axis, fmt="e4m3"):
    dtype, down = {"e4m3": (ml_dtypes.float8_e4m3fn, 7), "e5m2": (ml_dtypes.float8_e5m2, 14)}[fmt]
    v = np.moveaxis(np.asarray(x, np.float32).astype(ml_dtypes.bfloat16).astype(np.float64), axis, -1)
    blocks = v.reshape(v.shape[:-1] + (-1, 32))
    amax = np.abs(blocks).max(-1, keepdims=True)
    byte = np.maximum(np.where(amax > 0, np.frexp(amax)[1] - 1 + 127, 0) - down, 1)
    scale = np.exp2(byte - 127.0)
    codes = (blocks / scale).astype(np.float32).astype(dtype).astype(np.float64)
    return np.moveaxis((codes * scale).reshape(v.shape), -1, axis)


WIDE = False


def mx_kscale(k):
    if not WIDE:
        return np.ones(k)
    levels = np.array([10, -10, 5, -5, 0])
    if k % 512:
        return np.exp2(np.random.permutation(np.resize(levels, k // 32))).repeat(32)
    a = np.empty((k // 512, 16))
    for p in range(k // 512):
        a[p, :8] = np.random.permutation(np.resize(levels, 8))
        for g in range(8):
            far = levels[np.abs(levels - a[p, g]) >= 10]
            a[p, g + 8] = far[np.random.randint(len(far))]
    return np.exp2(a.ravel()).repeat(32)


BF16 = ml_dtypes.bfloat16


def bf(x):
    return np.asarray(x, np.float32).astype(BF16)


def f64(x):
    return np.asarray(x).astype(np.float64)


B, C, K, L, R = 4, 64, 1024, 4, 128


def transition():
    g = np.exp(2.5 * np.random.standard_normal((K, K)))
    return g / g.sum(1, keepdims=True)


def setup_inputs():
    s = mx_kscale(K)
    x = np.random.standard_normal((B, C, K, L)) * 2.0 * s[None, None, :, None]
    return {'x': bf(x.reshape(B, C, K * L)),
            'support0': bf(transition() * s[:, None] / s[None, :]),
            'support1': bf(transition() * s[:, None] / s[None, :])}


def two_hops(xq, a):
    aq = mxq(f64(a).T, 0, 'e4m3')
    x1 = xq @ aq
    x2 = mxq(x1, 2, 'e4m3') @ aq
    return x1, x2


def reference(x, support0, support1):
    xr = f64(x).reshape(B, C, K, L).transpose(0, 3, 1, 2).reshape(B * L, C, K)
    xq = mxq(xr, 2, 'e4m3')
    f1, f2 = two_hops(xq, support0)
    g1, g2 = two_hops(xq, support1)
    return f1, f2, g1, g2

@@ -1,0 +1,199 @@
+from contextlib import ExitStack
+
+import concourse.mybir as mybir
+from concourse.masks import make_identity
+
+F32 = mybir.dt.float32
+BF16 = mybir.dt.bfloat16
+U32 = mybir.dt.uint32
+U8 = mybir.dt.uint8
+FP8X4 = mybir.dt.float8_e4m3fn_x4
+
+P = 128
+PACK = 4
+PAIR = 2
+K_PASS = P * PACK
+NODES = 1024
+ROWS = 1024
+STEPS = 4
+CHANNELS = 64
+PASSES = NODES // K_PASS
+WIDE = 512
+HALVES = ROWS // WIDE
+TILES = WIDE // P
+
+FLOPS = 4 * 2 * ROWS * NODES * NODES
+
+
+def tile_adaptivegcn_pb_kernel(tc, x, support0, support1, out_0, out_1, out_2, out_3):
+    nc = tc.nc
+    supports = (support0, support1)
+    first_out = [o.rearrange("n c w -> (n c) w") for o in (out_0, out_2)]
+    second_out = [o.rearrange("n c w -> (n c) w") for o in (out_1, out_3)]
+
+    with ExitStack() as ctx:
+        keep = ctx.enter_context(tc.tile_pool(name="keep", bufs=1))
+        group_pool = ctx.enter_context(tc.tile_pool(name="group", bufs=4))
+        result_pool = ctx.enter_context(tc.tile_pool(name="result", bufs=6))
+        small_banks = ctx.enter_context(tc.psum_pool(name="small_banks", bufs=4))
+        wide_banks = ctx.enter_context(tc.psum_pool(name="wide_banks", bufs=4))
+
+        identity = keep.tile([P, P], F32, name="identity")
+        make_identity(nc, identity[:])
+
+        x_raw = [keep.tile([P, NODES * STEPS], BF16, name="x_raw%d" % r) for r in range(HALVES)]
+        x_steps = [keep.tile([P, STEPS, NODES], BF16, name="x_steps%d" % r) for r in range(HALVES)]
+        a_raw = [keep.tile([P, HALVES, PACK, NODES], BF16, name="a_raw%d" % s) for s in range(2)]
+
+        def mx_operand(name):
+            codes = keep.tile([P, PASSES, 1024], U32, name=name + "_codes", align_bytes=64)
+            scales = keep.tile([P, PASSES, 1024], U8, name=name + "_scales", align_bytes=64)
+            return codes, scales
+
+        x_mx = mx_operand("x")
+        a_mx = [mx_operand("a%d" % s) for s in range(2)]
+        hop_mx = [mx_operand("hop%d" % s) for s in range(2)]
+
+        x_rows = x.rearrange("b c f -> (b c) f")
+
+        def load_x(r):
+            for g in range(PASSES):
+                cols = slice(g * K_PASS * STEPS, (g + 1) * K_PASS * STEPS)
+                nc.sync.dma_start(out=x_raw[r][:, cols], in_=x_rows[r * P : (r + 1) * P, cols])
+
+        def load_support(s):
+            blocks = supports[s].rearrange("(g p t) v -> g p t v", p=P, t=PACK)
+            for g in range(HALVES):
+                for u in range(PAIR):
+                    pair = slice(PAIR * u, PAIR * (u + 1))
+                    nc.sync.dma_start(out=a_raw[s][:, g, pair, :], in_=blocks[g][:, pair, :])
+
+        load_x(0)
+        load_support(0)
+        load_x(1)
+        load_support(1)
+
+        def quantise(grouped, operand, g, cols):
+            codes, scales = operand
+            nc.vector.quantize_mx(
+                out=codes[:, g, cols].bitcast(FP8X4),
+                scales=scales[:, g, cols],
+                in_=grouped[:].rearrange("p c t -> p (c t)"),
+            )
+
+        def transpose_words(first, second, g):
+            bank = small_banks.tile([P, 2, PAIR, P], F32, tag="bank")
+            for a, view in enumerate((first, second)):
+                words = view.bitcast(F32)
+                for u in range(PAIR):
+                    start = PAIR * g * P + u
+                    every_second = words[:, start : start + PAIR * P - u : PAIR]
+                    nc.tensor.transpose(bank[:, a, u, :], every_second, identity[:])
+            return bank
+
+        def prepare_x(r):
+            for g in range(PASSES):
+                nodes = slice(g * K_PASS, (g + 1) * K_PASS)
+                nc.vector.tensor_copy(
+                    out=x_steps[r][:, :, nodes],
+                    in_=x_raw[r][:].rearrange("p (k l) -> p l k", l=STEPS)[:, :, nodes],
+                )
+            for g in range(PASSES):
+                grouped = group_pool.tile([P, WIDE, PACK], BF16, tag="grouped", align_bytes=64)
+                grouped_words = grouped[:].bitcast(F32)
+                for h in range(STEPS // 2):
+                    bank = transpose_words(x_steps[r][:, 2 * h, :], x_steps[r][:, 2 * h + 1, :], g)
+                    for b in range(2):
+                        first = (b * STEPS + 2 * h) * CHANNELS
+                        nc.scalar.copy(
+                            out=grouped_words[:, first : first + P, :].rearrange(
+                                "p (a c) u -> p a c u", a=2
+                            ),
+                            in_=bank[:, :, :, b * CHANNELS : (b + 1) * CHANNELS].rearrange(
+                                "p a u c -> p a c u"
+                            ),
+                        )
+                quantise(grouped, x_mx, g, slice(r * WIDE, (r + 1) * WIDE))
+
+        def prepare_support(s):
+            for half in range(HALVES):
+                for g in range(PASSES):
+                    grouped = group_pool.tile([P, WIDE, PACK], BF16, tag="grouped", align_bytes=64)
+                    grouped_words = grouped[:].bitcast(F32)
+                    for jj in range(2):
+                        bank = transpose_words(
+                            a_raw[s][:, half, 2 * jj, :], a_raw[s][:, half, 2 * jj + 1, :], g
+                        )
+                        nc.scalar.copy(
+                            out=grouped_words[:, jj * 2 * P : (jj + 1) * 2 * P, :].rearrange(
+                                "p (a c) u -> p a c u", a=2
+                            ),
+                            in_=bank[:].rearrange("p a u c -> p a c u"),
+                        )
+                    quantise(grouped, a_mx[s], g, slice(half * WIDE, (half + 1) * WIDE))
+
+        def copy_out(turn, out, in_):
+            if turn % 2 == 0:
+                nc.vector.tensor_copy(out=out, in_=in_)
+            else:
+                nc.scalar.copy(out=out, in_=in_)
+
+        def multiply(out, stationary, s_cols, moving, m_cols):
+            for g in range(PASSES):
+                nc.tensor.matmul_mx(
+                    out=out,
+                    lhsT=stationary[0][:, g, s_cols].bitcast(FP8X4),
+                    lhsT_scale=stationary[1][:, g, s_cols],
+                    rhs=moving[0][:, g, m_cols].bitcast(FP8X4),
+                    rhs_scale=moving[1][:, g, m_cols],
+                    start=(g == 0),
+                    stop=(g == PASSES - 1),
+                )
+
+        def first_hop_for_second(s, half):
+            for g in range(PASSES):
+                grouped = group_pool.tile([P, WIDE, PACK], BF16, tag="grouped", align_bytes=64)
+                for i in range(TILES):
+                    rows = slice(half * WIDE + i * P, half * WIDE + (i + 1) * P)
+                    bank = small_banks.tile([P, PACK, P], F32, tag="bank")
+                    for t in range(PACK):
+                        nodes = slice(g * K_PASS + t * P, g * K_PASS + (t + 1) * P)
+                        multiply(bank[:, t, :], a_mx[s], nodes, x_mx, rows)
+                    copy_out(
+                        i,
+                        grouped[:, i * P : (i + 1) * P, :],
+                        bank[:].rearrange("p t m -> p m t"),
+                    )
+                quantise(grouped, hop_mx[s], g, slice(half * WIDE, (half + 1) * WIDE))
+
+        def hop_to_output(operand, s, half, out):
+            for i in range(TILES):
+                rows = slice(half * WIDE + i * P, half * WIDE + (i + 1) * P)
+                result = result_pool.tile([P, NODES], F32, tag="result")
+                for g in range(HALVES):
+                    cols = slice(g * WIDE, (g + 1) * WIDE)
+                    bank = wide_banks.tile([P, WIDE], F32, tag="wide")
+                    multiply(bank[:], operand, rows, a_mx[s], cols)
+                    copy_out(
+                        g,
+                        result[:, cols].rearrange("m (p t) -> m p t", t=PACK),
+                        bank[:].rearrange("m (t p) -> m p t", t=PACK),
+                    )
+                nc.sync.dma_start(out=out[rows, :], in_=result[:])
+
+        prepare_x(0)
+        prepare_support(0)
+        first_hop_for_second(0, 0)
+        prepare_x(1)
+        hop_to_output(x_mx, 0, 0, first_out[0])
+        first_hop_for_second(0, 1)
+        prepare_support(1)
+        hop_to_output(x_mx, 0, 1, first_out[0])
+        hop_to_output(hop_mx[0], 0, 0, second_out[0])
+        first_hop_for_second(1, 0)
+        hop_to_output(hop_mx[0], 0, 1, second_out[0])
+        hop_to_output(x_mx, 1, 0, first_out[1])
+        first_hop_for_second(1, 1)
+        hop_to_output(x_mx, 1, 1, first_out[1])
+        hop_to_output(hop_mx[1], 1, 0, second_out[1])
+        hop_to_output(hop_mx[1], 1, 1, second_out[1])

@@ -34,25 +34,29 @@ def tile_adaptivegcn_pb_kernel(tc, x, support0, support1, out_0, out_1, out_2, o
     with ExitStack() as ctx:
         keep = ctx.enter_context(tc.tile_pool(name="keep", bufs=1))
         group_pool = ctx.enter_context(tc.tile_pool(name="group", bufs=4))
-        result_pool = ctx.enter_context(tc.tile_pool(name="result", bufs=6))
-        small_banks = ctx.enter_context(tc.psum_pool(name="small_banks", bufs=4))
-        wide_banks = ctx.enter_context(tc.psum_pool(name="wide_banks", bufs=4))
+        result_pool = ctx.enter_context(tc.tile_pool(name="result", bufs=8))
+        turned_banks = ctx.enter_context(tc.psum_pool(name="turned_banks", bufs=4))
+        product_banks = ctx.enter_context(tc.psum_pool(name="product_banks", bufs=4))
 
         identity = keep.tile([P, P], F32, name="identity")
         make_identity(nc, identity[:])
 
         x_raw = [keep.tile([P, NODES * STEPS], BF16, name="x_raw%d" % r) for r in range(HALVES)]
-        x_steps = [keep.tile([P, STEPS, NODES], BF16, name="x_steps%d" % r) for r in range(HALVES)]
-        a_raw = [keep.tile([P, HALVES, PACK, NODES], BF16, name="a_raw%d" % s) for s in range(2)]
+        a_raw = [keep.tile([P, NODES // P, NODES], BF16, name="a_raw%d" % s) for s in range(2)]
 
-        def mx_operand(name):
-            codes = keep.tile([P, PASSES, 1024], U32, name=name + "_codes", align_bytes=64)
-            scales = keep.tile([P, PASSES, 1024], U8, name=name + "_scales", align_bytes=64)
+        def row_operand(name):
+            codes = keep.tile([P, ROWS // P, PASSES, P], U32, name=name + "_codes", align_bytes=64)
+            scales = keep.tile([P, ROWS // P, PASSES, P], U8, name=name + "_scales", align_bytes=64)
             return codes, scales
 
-        x_mx = mx_operand("x")
-        a_mx = [mx_operand("a%d" % s) for s in range(2)]
-        hop_mx = [mx_operand("hop%d" % s) for s in range(2)]
+        def support_operand(name):
+            codes = keep.tile([P, HALVES, PASSES, WIDE], U32, name=name + "_codes", align_bytes=64)
+            scales = keep.tile([P, HALVES, PASSES, WIDE], U8, name=name + "_scales", align_bytes=64)
+            return codes, scales
+
+        x_mx = row_operand("x")
+        a_mx = [support_operand("a%d" % s) for s in range(2)]
+        hop_mx = [row_operand("hop%d" % s) for s in range(2)]
 
         x_rows = x.rearrange("b c f -> (b c) f")
 
@@ -62,138 +66,156 @@ def tile_adaptivegcn_pb_kernel(tc, x, support0, support1, out_0, out_1, out_2, o
                 nc.sync.dma_start(out=x_raw[r][:, cols], in_=x_rows[r * P : (r + 1) * P, cols])
 
         def load_support(s):
-            blocks = supports[s].rearrange("(g p t) v -> g p t v", p=P, t=PACK)
-            for g in range(HALVES):
-                for u in range(PAIR):
-                    pair = slice(PAIR * u, PAIR * (u + 1))
-                    nc.sync.dma_start(out=a_raw[s][:, g, pair, :], in_=blocks[g][:, pair, :])
+            blocks = supports[s].rearrange("(j p) v -> p j v", p=P)
+            for j in range(0, NODES // P, 2):
+                nc.sync.dma_start(out=a_raw[s][:, j : j + 2, :], in_=blocks[:, j : j + 2, :])
 
         load_x(0)
         load_support(0)
         load_x(1)
         load_support(1)
 
-        def quantise(grouped, operand, g, cols):
-            codes, scales = operand
-            nc.vector.quantize_mx(
-                out=codes[:, g, cols].bitcast(FP8X4),
-                scales=scales[:, g, cols],
-                in_=grouped[:].rearrange("p c t -> p (c t)"),
-            )
-
-        def transpose_words(first, second, g):
-            bank = small_banks.tile([P, 2, PAIR, P], F32, tag="bank")
-            for a, view in enumerate((first, second)):
-                words = view.bitcast(F32)
-                for u in range(PAIR):
-                    start = PAIR * g * P + u
-                    every_second = words[:, start : start + PAIR * P - u : PAIR]
-                    nc.tensor.transpose(bank[:, a, u, :], every_second, identity[:])
-            return bank
-
-        def prepare_x(r):
-            for g in range(PASSES):
-                nodes = slice(g * K_PASS, (g + 1) * K_PASS)
-                nc.vector.tensor_copy(
-                    out=x_steps[r][:, :, nodes],
-                    in_=x_raw[r][:].rearrange("p (k l) -> p l k", l=STEPS)[:, :, nodes],
-                )
-            for g in range(PASSES):
-                grouped = group_pool.tile([P, WIDE, PACK], BF16, tag="grouped", align_bytes=64)
-                grouped_words = grouped[:].bitcast(F32)
-                for h in range(STEPS // 2):
-                    bank = transpose_words(x_steps[r][:, 2 * h, :], x_steps[r][:, 2 * h + 1, :], g)
-                    for b in range(2):
-                        first = (b * STEPS + 2 * h) * CHANNELS
-                        nc.scalar.copy(
-                            out=grouped_words[:, first : first + P, :].rearrange(
-                                "p (a c) u -> p a c u", a=2
-                            ),
-                            in_=bank[:, :, :, b * CHANNELS : (b + 1) * CHANNELS].rearrange(
-                                "p a u c -> p a c u"
-                            ),
-                        )
-                quantise(grouped, x_mx, g, slice(r * WIDE, (r + 1) * WIDE))
-
-        def prepare_support(s):
-            for half in range(HALVES):
-                for g in range(PASSES):
-                    grouped = group_pool.tile([P, WIDE, PACK], BF16, tag="grouped", align_bytes=64)
-                    grouped_words = grouped[:].bitcast(F32)
-                    for jj in range(2):
-                        bank = transpose_words(
-                            a_raw[s][:, half, 2 * jj, :], a_raw[s][:, half, 2 * jj + 1, :], g
-                        )
-                        nc.scalar.copy(
-                            out=grouped_words[:, jj * 2 * P : (jj + 1) * 2 * P, :].rearrange(
-                                "p (a c) u -> p a c u", a=2
-                            ),
-                            in_=bank[:].rearrange("p a u c -> p a c u"),
-                        )
-                    quantise(grouped, a_mx[s], g, slice(half * WIDE, (half + 1) * WIDE))
-
-        def copy_out(turn, out, in_):
-            if turn % 2 == 0:
+        def copy_out(on_vector, out, in_):
+            if on_vector:
                 nc.vector.tensor_copy(out=out, in_=in_)
             else:
                 nc.scalar.copy(out=out, in_=in_)
 
-        def multiply(out, stationary, s_cols, moving, m_cols):
+        def prepare_x(r):
+            words = x_raw[r][:].bitcast(F32)
+            for h in range(STEPS // 2):
+                grouped = group_pool.tile([P, 2, PASSES, P, PACK], BF16, tag="grouped", align_bytes=64)
+                for g in range(PASSES):
+                    bank = turned_banks.tile([P, PACK, P], F32, tag="turned")
+                    for t in range(PACK):
+                        start = 2 * (g * K_PASS + t) + h
+                        stop = start + 2 * PACK * (P - 1) + 1
+                        nc.tensor.transpose(
+                            bank[:, t, :], words[:, start : stop : 2 * PACK], identity[:]
+                        )
+                    values = bank[:].rearrange("p t i -> p (t i)").bitcast(BF16)
+                    copy_out(
+                        g == 0,
+                        grouped[:, :, g, :, :].rearrange("p b (o c) t -> p b o c t", o=2),
+                        values.rearrange("p (t b c o) -> p b o c t", t=PACK, b=2, o=2),
+                    )
+                for b in range(2):
+                    tile = (2 * r + b) * 2 + h
+                    nc.vector.quantize_mx(
+                        out=x_mx[0][:, tile, :, :].rearrange("p g m -> p (g m)").bitcast(FP8X4),
+                        scales=x_mx[1][:, tile, :, :].rearrange("p g m -> p (g m)"),
+                        in_=grouped[:, b, :, :, :].rearrange("p g m t -> p (g m t)"),
+                    )
+
+        def prepare_support(s, half):
+            for g in range(PASSES):
+                grouped = group_pool.tile([P, WIDE, PACK], BF16, tag="grouped", align_bytes=64)
+                grouped_words = grouped[:].bitcast(F32)
+                for jj in range(2):
+                    bank = turned_banks.tile([P, 2, PAIR, P], F32, tag="turned")
+                    for a in range(2):
+                        words = a_raw[s][:, TILES * half + 2 * jj + a, :].bitcast(F32)
+                        for u in range(PAIR):
+                            start = PAIR * g * P + u
+                            stop = start + PAIR * (P - 1) + 1
+                            nc.tensor.transpose(
+                                bank[:, a, u, :], words[:, start : stop : PAIR], identity[:]
+                            )
+                    copy_out(
+                        jj == 0,
+                        grouped_words[:, jj * 2 * P : (jj + 1) * 2 * P, :].rearrange(
+                            "p (a c) u -> p a c u", a=2
+                        ),
+                        bank[:].rearrange("p a u c -> p a c u"),
+                    )
+                nc.vector.quantize_mx(
+                    out=a_mx[s][0][:, half, g, :].bitcast(FP8X4),
+                    scales=a_mx[s][1][:, half, g, :],
+                    in_=grouped[:].rearrange("p c t -> p (c t)"),
+                )
+
+        def multiply(rows_mx, tile, s, half):
+            bank = product_banks.tile([P, WIDE], F32, tag="product")
             for g in range(PASSES):
                 nc.tensor.matmul_mx(
-                    out=out,
-                    lhsT=stationary[0][:, g, s_cols].bitcast(FP8X4),
-                    lhsT_scale=stationary[1][:, g, s_cols],
-                    rhs=moving[0][:, g, m_cols].bitcast(FP8X4),
-                    rhs_scale=moving[1][:, g, m_cols],
+                    out=bank[:],
+                    lhsT=rows_mx[0][:, tile, g, :].bitcast(FP8X4),
+                    lhsT_scale=rows_mx[1][:, tile, g, :],
+                    rhs=a_mx[s][0][:, half, g, :].bitcast(FP8X4),
+                    rhs_scale=a_mx[s][1][:, half, g, :],
                     start=(g == 0),
                     stop=(g == PASSES - 1),
                 )
+            return bank
 
-        def first_hop_for_second(s, half):
-            for g in range(PASSES):
-                grouped = group_pool.tile([P, WIDE, PACK], BF16, tag="grouped", align_bytes=64)
-                for i in range(TILES):
-                    rows = slice(half * WIDE + i * P, half * WIDE + (i + 1) * P)
-                    bank = small_banks.tile([P, PACK, P], F32, tag="bank")
-                    for t in range(PACK):
-                        nodes = slice(g * K_PASS + t * P, g * K_PASS + (t + 1) * P)
-                        multiply(bank[:, t, :], a_mx[s], nodes, x_mx, rows)
-                    copy_out(
-                        i,
-                        grouped[:, i * P : (i + 1) * P, :],
-                        bank[:].rearrange("p t m -> p m t"),
-                    )
-                quantise(grouped, hop_mx[s], g, slice(half * WIDE, (half + 1) * WIDE))
+        rounded = {}
 
-        def hop_to_output(operand, s, half, out):
-            for i in range(TILES):
-                rows = slice(half * WIDE + i * P, half * WIDE + (i + 1) * P)
-                result = result_pool.tile([P, NODES], F32, tag="result")
-                for g in range(HALVES):
-                    cols = slice(g * WIDE, (g + 1) * WIDE)
-                    bank = wide_banks.tile([P, WIDE], F32, tag="wide")
-                    multiply(bank[:], operand, rows, a_mx[s], cols)
+        def first_hop(s, tile):
+            result = result_pool.tile([P, NODES], F32, tag="result")
+            for half in range(HALVES):
+                bank = multiply(x_mx, tile, s, half)
+                copy_out(False, result[:, half * WIDE : (half + 1) * WIDE], bank[:])
+            nc.sync.dma_start(out=first_out[s][tile * P : (tile + 1) * P, :], in_=result[:])
+            low = result_pool.tile([P, NODES], BF16, tag="rounded")
+            nc.vector.tensor_copy(
+                out=low[:].rearrange("m (g u q e) -> m g u q e", g=PASSES, u=PAIR, e=PAIR),
+                in_=result[:].rearrange("m (g q u e) -> m g u q e", g=PASSES, u=PAIR, e=PAIR),
+            )
+            rounded[s, tile] = low
+
+        def turn_hop(s, r):
+            for first in range(TILES * r, TILES * (r + 1), 2):
+                grouped = group_pool.tile([P, 2, PASSES, P, PACK], BF16, tag="grouped", align_bytes=64)
+                for a in range(2):
+                    words = rounded[s, first + a][:].bitcast(F32)
+                    bank = turned_banks.tile([P, PASSES, PAIR, P], F32, tag="turned")
+                    for g in range(PASSES):
+                        for u in range(PAIR):
+                            start = (PAIR * g + u) * P
+                            nc.tensor.transpose(bank[:, g, u, :], words[:, start : start + P], identity[:])
                     copy_out(
-                        g,
-                        result[:, cols].rearrange("m (p t) -> m p t", t=PACK),
-                        bank[:].rearrange("m (t p) -> m p t", t=PACK),
+                        a == 0,
+                        grouped[:, a, :, :, :].rearrange("p g c t -> p g (c t)").bitcast(F32).rearrange(
+                            "p g (c u) -> p g c u", u=PAIR
+                        ),
+                        bank[:].rearrange("p g u c -> p g c u"),
                     )
-                nc.sync.dma_start(out=out[rows, :], in_=result[:])
+                nc.vector.quantize_mx(
+                    out=hop_mx[s][0][:, first : first + 2, :, :].rearrange("p a g m -> p (a g m)").bitcast(FP8X4),
+                    scales=hop_mx[s][1][:, first : first + 2, :, :].rearrange("p a g m -> p (a g m)"),
+                    in_=grouped[:].rearrange("p a g m t -> p (a g m t)"),
+                )
+
+        def second_hop(s, tile):
+            result = result_pool.tile([P, NODES], F32, tag="result")
+            for half in range(HALVES):
+                bank = multiply(hop_mx[s], tile, s, half)
+                copy_out(half == 0, result[:, half * WIDE : (half + 1) * WIDE], bank[:])
+            nc.sync.dma_start(out=second_out[s][tile * P : (tile + 1) * P, :], in_=result[:])
+
+        def first_hops(s, r):
+            for tile in range(TILES * r, TILES * (r + 1)):
+                first_hop(s, tile)
+
+        def second_hops(s, r):
+            for tile in range(TILES * r, TILES * (r + 1)):
+                second_hop(s, tile)
 
         prepare_x(0)
-        prepare_support(0)
-        first_hop_for_second(0, 0)
+        prepare_support(0, 0)
+        prepare_support(0, 1)
+        first_hops(0, 0)
         prepare_x(1)
-        hop_to_output(x_mx, 0, 0, first_out[0])
-        first_hop_for_second(0, 1)
-        prepare_support(1)
-        hop_to_output(x_mx, 0, 1, first_out[0])
-        hop_to_output(hop_mx[0], 0, 0, second_out[0])
-        first_hop_for_second(1, 0)
-        hop_to_output(hop_mx[0], 0, 1, second_out[0])
-        hop_to_output(x_mx, 1, 0, first_out[1])
-        first_hop_for_second(1, 1)
-        hop_to_output(x_mx, 1, 1, first_out[1])
-        hop_to_output(hop_mx[1], 1, 0, second_out[1])
-        hop_to_output(hop_mx[1], 1, 1, second_out[1])
+        turn_hop(0, 0)
+        first_hops(0, 1)
+        prepare_support(1, 0)
+        second_hops(0, 0)
+        prepare_support(1, 1)
+        turn_hop(0, 1)
+        first_hops(1, 0)
+        second_hops(0, 1)
+        turn_hop(1, 0)
+        first_hops(1, 1)
+        second_hops(1, 0)
+        turn_hop(1, 1)
+        second_hops(1, 1)

@@ -81,7 +81,7 @@ def tile_adaptivegcn_pb_kernel(tc, x, support0, support1, out_0, out_1, out_2, o
             else:
                 nc.scalar.copy(out=out, in_=in_)
 
-        def prepare_x(r):
+        def prepare_x(r, on_vector):
             words = x_raw[r][:].bitcast(F32)
             for h in range(STEPS // 2):
                 grouped = group_pool.tile([P, 2, PASSES, P, PACK], BF16, tag="grouped", align_bytes=64)
@@ -95,7 +95,7 @@ def tile_adaptivegcn_pb_kernel(tc, x, support0, support1, out_0, out_1, out_2, o
                         )
                     values = bank[:].rearrange("p t i -> p (t i)").bitcast(BF16)
                     copy_out(
-                        g == 0,
+                        on_vector[h][g],
                         grouped[:, :, g, :, :].rearrange("p b (o c) t -> p b o c t", o=2),
                         values.rearrange("p (t b c o) -> p b o c t", t=PACK, b=2, o=2),
                     )
@@ -107,7 +107,7 @@ def tile_adaptivegcn_pb_kernel(tc, x, support0, support1, out_0, out_1, out_2, o
                         in_=grouped[:, b, :, :, :].rearrange("p g m t -> p (g m t)"),
                     )
 
-        def prepare_support(s, half):
+        def prepare_support(s, half, on_vector):
             for g in range(PASSES):
                 grouped = group_pool.tile([P, WIDE, PACK], BF16, tag="grouped", align_bytes=64)
                 grouped_words = grouped[:].bitcast(F32)
@@ -122,7 +122,7 @@ def tile_adaptivegcn_pb_kernel(tc, x, support0, support1, out_0, out_1, out_2, o
                                 bank[:, a, u, :], words[:, start : stop : PAIR], identity[:]
                             )
                     copy_out(
-                        jj == 0,
+                        on_vector[jj],
                         grouped_words[:, jj * 2 * P : (jj + 1) * 2 * P, :].rearrange(
                             "p (a c) u -> p a c u", a=2
                         ),
@@ -149,6 +149,17 @@ def tile_adaptivegcn_pb_kernel(tc, x, support0, support1, out_0, out_1, out_2, o
             return bank
 
         rounded = {}
+        waiting = []
+
+        def round_waiting():
+            for s, tile, result in waiting:
+                low = result_pool.tile([P, NODES], BF16, tag="rounded")
+                nc.vector.tensor_copy(
+                    out=low[:].rearrange("m (g u q e) -> m g u q e", g=PASSES, u=PAIR, e=PAIR),
+                    in_=result[:].rearrange("m (g q u e) -> m g u q e", g=PASSES, u=PAIR, e=PAIR),
+                )
+                rounded[s, tile] = low
+            waiting.clear()
 
         def first_hop(s, tile):
             result = result_pool.tile([P, NODES], F32, tag="result")
@@ -156,14 +167,11 @@ def tile_adaptivegcn_pb_kernel(tc, x, support0, support1, out_0, out_1, out_2, o
                 bank = multiply(x_mx, tile, s, half)
                 copy_out(False, result[:, half * WIDE : (half + 1) * WIDE], bank[:])
             nc.sync.dma_start(out=first_out[s][tile * P : (tile + 1) * P, :], in_=result[:])
-            low = result_pool.tile([P, NODES], BF16, tag="rounded")
-            nc.vector.tensor_copy(
-                out=low[:].rearrange("m (g u q e) -> m g u q e", g=PASSES, u=PAIR, e=PAIR),
-                in_=result[:].rearrange("m (g q u e) -> m g u q e", g=PASSES, u=PAIR, e=PAIR),
-            )
-            rounded[s, tile] = low
+            round_waiting()
+            waiting.append((s, tile, result))
 
         def turn_hop(s, r):
+            round_waiting()
             for first in range(TILES * r, TILES * (r + 1), 2):
                 grouped = group_pool.tile([P, 2, PASSES, P, PACK], BF16, tag="grouped", align_bytes=64)
                 for a in range(2):
@@ -192,30 +200,35 @@ def tile_adaptivegcn_pb_kernel(tc, x, support0, support1, out_0, out_1, out_2, o
                 bank = multiply(hop_mx[s], tile, s, half)
                 copy_out(half == 0, result[:, half * WIDE : (half + 1) * WIDE], bank[:])
             nc.sync.dma_start(out=second_out[s][tile * P : (tile + 1) * P, :], in_=result[:])
+            round_waiting()
 
-        def first_hops(s, r):
-            for tile in range(TILES * r, TILES * (r + 1)):
+        def first_hops(s, *tiles):
+            for tile in tiles:
                 first_hop(s, tile)
 
-        def second_hops(s, r):
-            for tile in range(TILES * r, TILES * (r + 1)):
+        def second_hops(s, *tiles):
+            for tile in tiles:
                 second_hop(s, tile)
 
-        prepare_x(0)
-        prepare_support(0, 0)
-        prepare_support(0, 1)
-        first_hops(0, 0)
-        prepare_x(1)
+        mostly_scalar = ((False, True), (False, True))
+        prepare_x(0, mostly_scalar)
+        prepare_support(0, 0, (False, False))
+        prepare_support(0, 1, (False, False))
+        first_hops(0, 0, 1)
+        prepare_x(1, mostly_scalar)
+        first_hops(0, 2, 3, 4)
         turn_hop(0, 0)
-        first_hops(0, 1)
-        prepare_support(1, 0)
+        first_hops(0, 5, 6, 7)
         second_hops(0, 0)
-        prepare_support(1, 1)
+        prepare_support(1, 0, (True, False))
+        second_hops(0, 1, 2)
         turn_hop(0, 1)
-        first_hops(1, 0)
-        second_hops(0, 1)
+        prepare_support(1, 1, (True, False))
+        second_hops(0, 3, 4, 5, 6)
+        first_hops(1, 0, 1, 2, 3)
+        second_hops(0, 7)
         turn_hop(1, 0)
-        first_hops(1, 1)
+        first_hops(1, 4, 5, 6, 7)
         second_hops(1, 0)
         turn_hop(1, 1)
-        second_hops(1, 1)
+        second_hops(1, 1, 2, 3, 4, 5, 6, 7)

@@ -34,15 +34,14 @@ def tile_adaptivegcn_pb_kernel(tc, x, support0, support1, out_0, out_1, out_2, o
     with ExitStack() as ctx:
         keep = ctx.enter_context(tc.tile_pool(name="keep", bufs=1))
         group_pool = ctx.enter_context(tc.tile_pool(name="group", bufs=4))
-        result_pool = ctx.enter_context(tc.tile_pool(name="result", bufs=8))
-        turned_banks = ctx.enter_context(tc.psum_pool(name="turned_banks", bufs=4))
-        product_banks = ctx.enter_context(tc.psum_pool(name="product_banks", bufs=4))
+        result_pool = ctx.enter_context(tc.tile_pool(name="result", bufs=14))
+        banks = ctx.enter_context(tc.psum_pool(name="banks", bufs=8))
 
         identity = keep.tile([P, P], F32, name="identity")
         make_identity(nc, identity[:])
 
         x_raw = [keep.tile([P, NODES * STEPS], BF16, name="x_raw%d" % r) for r in range(HALVES)]
-        a_raw = [keep.tile([P, NODES // P, NODES], BF16, name="a_raw%d" % s) for s in range(2)]
+        a_raw = [keep.tile([P, HALVES, PACK, NODES], BF16, name="a_raw%d" % s) for s in range(2)]
 
         def row_operand(name):
             codes = keep.tile([P, ROWS // P, PASSES, P], U32, name=name + "_codes", align_bytes=64)
@@ -66,9 +65,12 @@ def tile_adaptivegcn_pb_kernel(tc, x, support0, support1, out_0, out_1, out_2, o
                 nc.sync.dma_start(out=x_raw[r][:, cols], in_=x_rows[r * P : (r + 1) * P, cols])
 
         def load_support(s):
-            blocks = supports[s].rearrange("(j p) v -> p j v", p=P)
-            for j in range(0, NODES // P, 2):
-                nc.sync.dma_start(out=a_raw[s][:, j : j + 2, :], in_=blocks[:, j : j + 2, :])
+            blocks = supports[s].rearrange("(h p t) v -> h p t v", p=P, t=PACK)
+            for half in range(HALVES):
+                for t in range(0, PACK, 2):
+                    nc.sync.dma_start(
+                        out=a_raw[s][:, half, t : t + 2, :], in_=blocks[half][:, t : t + 2, :]
+                    )
 
         load_x(0)
         load_support(0)
@@ -81,12 +83,19 @@ def tile_adaptivegcn_pb_kernel(tc, x, support0, support1, out_0, out_1, out_2, o
             else:
                 nc.scalar.copy(out=out, in_=in_)
 
+        def copy_result(on_vector, result, half, bank):
+            copy_out(
+                on_vector,
+                result[:, half * WIDE : (half + 1) * WIDE].rearrange("m (p t) -> m p t", t=PACK),
+                bank[:].rearrange("m (t p) -> m p t", t=PACK),
+            )
+
         def prepare_x(r, on_vector):
             words = x_raw[r][:].bitcast(F32)
             for h in range(STEPS // 2):
                 grouped = group_pool.tile([P, 2, PASSES, P, PACK], BF16, tag="grouped", align_bytes=64)
                 for g in range(PASSES):
-                    bank = turned_banks.tile([P, PACK, P], F32, tag="turned")
+                    bank = banks.tile([P, PACK, P], F32, tag="bank")
                     for t in range(PACK):
                         start = 2 * (g * K_PASS + t) + h
                         stop = start + 2 * PACK * (P - 1) + 1
@@ -112,9 +121,9 @@ def tile_adaptivegcn_pb_kernel(tc, x, support0, support1, out_0, out_1, out_2, o
                 grouped = group_pool.tile([P, WIDE, PACK], BF16, tag="grouped", align_bytes=64)
                 grouped_words = grouped[:].bitcast(F32)
                 for jj in range(2):
-                    bank = turned_banks.tile([P, 2, PAIR, P], F32, tag="turned")
+                    bank = banks.tile([P, 2, PAIR, P], F32, tag="bank")
                     for a in range(2):
-                        words = a_raw[s][:, TILES * half + 2 * jj + a, :].bitcast(F32)
+                        words = a_raw[s][:, half, 2 * jj + a, :].bitcast(F32)
                         for u in range(PAIR):
                             start = PAIR * g * P + u
                             stop = start + PAIR * (P - 1) + 1
@@ -135,7 +144,7 @@ def tile_adaptivegcn_pb_kernel(tc, x, support0, support1, out_0, out_1, out_2, o
                 )
 
         def multiply(rows_mx, tile, s, half):
-            bank = product_banks.tile([P, WIDE], F32, tag="product")
+            bank = banks.tile([P, WIDE], F32, tag="bank")
             for g in range(PASSES):
                 nc.tensor.matmul_mx(
                     out=bank[:],
@@ -149,34 +158,32 @@ def tile_adaptivegcn_pb_kernel(tc, x, support0, support1, out_0, out_1, out_2, o
             return bank
 
         rounded = {}
-        waiting = []
+        results = {}
 
-        def round_waiting():
-            for s, tile, result in waiting:
+        def round_hop(s, r):
+            for tile in range(TILES * r, TILES * (r + 1)):
+                result = results[s, tile]
                 low = result_pool.tile([P, NODES], BF16, tag="rounded")
                 nc.vector.tensor_copy(
                     out=low[:].rearrange("m (g u q e) -> m g u q e", g=PASSES, u=PAIR, e=PAIR),
                     in_=result[:].rearrange("m (g q u e) -> m g u q e", g=PASSES, u=PAIR, e=PAIR),
                 )
                 rounded[s, tile] = low
-            waiting.clear()
 
         def first_hop(s, tile):
             result = result_pool.tile([P, NODES], F32, tag="result")
             for half in range(HALVES):
                 bank = multiply(x_mx, tile, s, half)
-                copy_out(False, result[:, half * WIDE : (half + 1) * WIDE], bank[:])
+                copy_result(False, result, half, bank)
             nc.sync.dma_start(out=first_out[s][tile * P : (tile + 1) * P, :], in_=result[:])
-            round_waiting()
-            waiting.append((s, tile, result))
+            results[s, tile] = result
 
         def turn_hop(s, r):
-            round_waiting()
             for first in range(TILES * r, TILES * (r + 1), 2):
                 grouped = group_pool.tile([P, 2, PASSES, P, PACK], BF16, tag="grouped", align_bytes=64)
                 for a in range(2):
                     words = rounded[s, first + a][:].bitcast(F32)
-                    bank = turned_banks.tile([P, PASSES, PAIR, P], F32, tag="turned")
+                    bank = banks.tile([P, PASSES, PAIR, P], F32, tag="bank")
                     for g in range(PASSES):
                         for u in range(PAIR):
                             start = (PAIR * g + u) * P
@@ -198,9 +205,8 @@ def tile_adaptivegcn_pb_kernel(tc, x, support0, support1, out_0, out_1, out_2, o
             result = result_pool.tile([P, NODES], F32, tag="result")
             for half in range(HALVES):
                 bank = multiply(hop_mx[s], tile, s, half)
-                copy_out(half == 0, result[:, half * WIDE : (half + 1) * WIDE], bank[:])
+                copy_result(half == 0, result, half, bank)
             nc.sync.dma_start(out=second_out[s][tile * P : (tile + 1) * P, :], in_=result[:])
-            round_waiting()
 
         def first_hops(s, *tiles):
             for tile in tiles:
@@ -216,19 +222,20 @@ def tile_adaptivegcn_pb_kernel(tc, x, support0, support1, out_0, out_1, out_2, o
         prepare_support(0, 1, (False, False))
         first_hops(0, 0, 1)
         prepare_x(1, mostly_scalar)
-        first_hops(0, 2, 3, 4)
-        turn_hop(0, 0)
-        first_hops(0, 5, 6, 7)
-        second_hops(0, 0)
+        first_hops(0, 2, 3, 4, 5)
         prepare_support(1, 0, (True, False))
-        second_hops(0, 1, 2)
-        turn_hop(0, 1)
+        first_hops(0, 6, 7)
         prepare_support(1, 1, (True, False))
-        second_hops(0, 3, 4, 5, 6)
+        round_hop(0, 0)
         first_hops(1, 0, 1, 2, 3)
-        second_hops(0, 7)
-        turn_hop(1, 0)
+        turn_hop(0, 0)
+        round_hop(0, 1)
         first_hops(1, 4, 5, 6, 7)
-        second_hops(1, 0)
+        turn_hop(0, 1)
+        round_hop(1, 0)
+        second_hops(0, 0, 1, 2, 3)
+        turn_hop(1, 0)
+        round_hop(1, 1)
+        second_hops(0, 4, 5, 6, 7)
         turn_hop(1, 1)
-        second_hops(1, 1, 2, 3, 4, 5, 6, 7)
+        second_hops(1, 0, 1, 2, 3, 4, 5, 6, 7)

@@ -34,11 +34,18 @@ def tile_adaptivegcn_pb_kernel(tc, x, support0, support1, out_0, out_1, out_2, o
     with ExitStack() as ctx:
         keep = ctx.enter_context(tc.tile_pool(name="keep", bufs=1))
         group_pool = ctx.enter_context(tc.tile_pool(name="group", bufs=4))
+        sorted_pool = ctx.enter_context(tc.tile_pool(name="sorted", bufs=2))
         result_pool = ctx.enter_context(tc.tile_pool(name="result", bufs=14))
+        pair_pool = ctx.enter_context(tc.tile_pool(name="pair", bufs=8))
         banks = ctx.enter_context(tc.psum_pool(name="banks", bufs=8))
 
         identity = keep.tile([P, P], F32, name="identity")
         make_identity(nc, identity[:])
+        sorting = keep.tile([P, P], F32, name="sorting")
+        nc.vector.tensor_copy(
+            out=sorting[:].rearrange("p (b a c) -> p b a c", b=2, a=PAIR),
+            in_=identity[:].rearrange("p (b c a) -> p b a c", b=2, a=PAIR),
+        )
 
         x_raw = [keep.tile([P, NODES * STEPS], BF16, name="x_raw%d" % r) for r in range(HALVES)]
         a_raw = [keep.tile([P, HALVES, PACK, NODES], BF16, name="a_raw%d" % s) for s in range(2)]
@@ -64,18 +71,21 @@ def tile_adaptivegcn_pb_kernel(tc, x, support0, support1, out_0, out_1, out_2, o
                 cols = slice(g * K_PASS * STEPS, (g + 1) * K_PASS * STEPS)
                 nc.sync.dma_start(out=x_raw[r][:, cols], in_=x_rows[r * P : (r + 1) * P, cols])
 
-        def load_support(s):
-            blocks = supports[s].rearrange("(h p t) v -> h p t v", p=P, t=PACK)
+        def load_support(s, pieces):
+            blocks = supports[s].rearrange("(h p t) v -> h p (t v)", p=P, t=PACK)
+            length = PACK * NODES // pieces
             for half in range(HALVES):
-                for t in range(0, PACK, 2):
+                run = a_raw[s][:, half, :, :].rearrange("p t v -> p (t v)")
+                for start in range(0, PACK * NODES, length):
                     nc.sync.dma_start(
-                        out=a_raw[s][:, half, t : t + 2, :], in_=blocks[half][:, t : t + 2, :]
+                        out=run[:, start : start + length],
+                        in_=blocks[half][:, start : start + length],
                     )
 
         load_x(0)
-        load_support(0)
+        load_support(0, 2)
         load_x(1)
-        load_support(1)
+        load_support(1, 1)
 
         def copy_out(on_vector, out, in_):
             if on_vector:
@@ -92,29 +102,33 @@ def tile_adaptivegcn_pb_kernel(tc, x, support0, support1, out_0, out_1, out_2, o
 
         def prepare_x(r, on_vector):
             words = x_raw[r][:].bitcast(F32)
+            grouped = sorted_pool.tile(
+                [P, 2 * PAIR, PASSES, STEPS, CHANNELS // PAIR, PACK], BF16, tag="sorted", align_bytes=64
+            )
             for h in range(STEPS // 2):
-                grouped = group_pool.tile([P, 2, PASSES, P, PACK], BF16, tag="grouped", align_bytes=64)
                 for g in range(PASSES):
                     bank = banks.tile([P, PACK, P], F32, tag="bank")
                     for t in range(PACK):
                         start = 2 * (g * K_PASS + t) + h
                         stop = start + 2 * PACK * (P - 1) + 1
                         nc.tensor.transpose(
-                            bank[:, t, :], words[:, start : stop : 2 * PACK], identity[:]
+                            bank[:, t, :], words[:, start : stop : 2 * PACK], sorting[:]
                         )
                     values = bank[:].rearrange("p t i -> p (t i)").bitcast(BF16)
                     copy_out(
                         on_vector[h][g],
-                        grouped[:, :, g, :, :].rearrange("p b (o c) t -> p b o c t", o=2),
-                        values.rearrange("p (t b c o) -> p b o c t", t=PACK, b=2, o=2),
+                        grouped[:, :, g, 2 * h : 2 * h + 2, :, :],
+                        values.rearrange("p (t a c o) -> p a o c t", t=PACK, a=2 * PAIR, o=2),
                     )
-                for b in range(2):
-                    tile = (2 * r + b) * 2 + h
-                    nc.vector.quantize_mx(
-                        out=x_mx[0][:, tile, :, :].rearrange("p g m -> p (g m)").bitcast(FP8X4),
-                        scales=x_mx[1][:, tile, :, :].rearrange("p g m -> p (g m)"),
-                        in_=grouped[:, b, :, :, :].rearrange("p g m t -> p (g m t)"),
-                    )
+            for b in range(2):
+                tiles = slice(TILES * r + PAIR * b, TILES * r + PAIR * (b + 1))
+                nc.vector.quantize_mx(
+                    out=x_mx[0][:, tiles, :, :].rearrange("p a g m -> p (a g m)").bitcast(FP8X4),
+                    scales=x_mx[1][:, tiles, :, :].rearrange("p a g m -> p (a g m)"),
+                    in_=grouped[:, PAIR * b : PAIR * (b + 1), :, :, :, :].rearrange(
+                        "p a g l c t -> p (a g l c t)"
+                    ),
+                )
 
         def prepare_support(s, half, on_vector):
             for g in range(PASSES):
@@ -166,16 +180,36 @@ def tile_adaptivegcn_pb_kernel(tc, x, support0, support1, out_0, out_1, out_2, o
                 low = result_pool.tile([P, NODES], BF16, tag="rounded")
                 nc.vector.tensor_copy(
                     out=low[:].rearrange("m (g u q e) -> m g u q e", g=PASSES, u=PAIR, e=PAIR),
-                    in_=result[:].rearrange("m (g q u e) -> m g u q e", g=PASSES, u=PAIR, e=PAIR),
+                    in_=result.rearrange("m (g q u e) -> m g u q e", g=PASSES, u=PAIR, e=PAIR),
                 )
                 rounded[s, tile] = low
 
+        def open_result(tile, open_pairs):
+            if tile % PAIR == 0:
+                open_pairs[0] = pair_pool.tile([P, PAIR, NODES], F32, tag="pair", name="pair")
+            return open_pairs[0][:, tile % PAIR, :]
+
+        def store(out, tile, pair, together):
+            rows = out[tile // PAIR * PAIR * P : (tile // PAIR + 1) * PAIR * P, :]
+            if not together:
+                nc.sync.dma_start(
+                    out=rows.rearrange("(m a) w -> m a w", a=PAIR)[:, tile % PAIR, :],
+                    in_=pair[:, tile % PAIR, :],
+                )
+            elif tile % PAIR == PAIR - 1:
+                nc.sync.dma_start(
+                    out=rows.rearrange("(m a) w -> m (a w)", a=PAIR),
+                    in_=pair[:].rearrange("p a w -> p (a w)"),
+                )
+
+        open_pair = [None]
+
         def first_hop(s, tile):
-            result = result_pool.tile([P, NODES], F32, tag="result")
+            result = open_result(tile, open_pair)
             for half in range(HALVES):
                 bank = multiply(x_mx, tile, s, half)
                 copy_result(False, result, half, bank)
-            nc.sync.dma_start(out=first_out[s][tile * P : (tile + 1) * P, :], in_=result[:])
+            store(first_out[s], tile, open_pair[0], together=(s == 1))
             results[s, tile] = result
 
         def turn_hop(s, r):
@@ -202,11 +236,12 @@ def tile_adaptivegcn_pb_kernel(tc, x, support0, support1, out_0, out_1, out_2, o
                 )
 
         def second_hop(s, tile):
-            result = result_pool.tile([P, NODES], F32, tag="result")
+            result = open_result(tile, open_pair)
             for half in range(HALVES):
                 bank = multiply(hop_mx[s], tile, s, half)
                 copy_result(half == 0, result, half, bank)
-            nc.sync.dma_start(out=second_out[s][tile * P : (tile + 1) * P, :], in_=result[:])
+            last = s == 1 and tile >= ROWS // P - PAIR
+            store(second_out[s], tile, open_pair[0], together=not last)
 
         def first_hops(s, *tiles):
             for tile in tiles:
@@ -220,12 +255,12 @@ def tile_adaptivegcn_pb_kernel(tc, x, support0, support1, out_0, out_1, out_2, o
         prepare_x(0, mostly_scalar)
         prepare_support(0, 0, (False, False))
         prepare_support(0, 1, (False, False))
-        first_hops(0, 0, 1)
         prepare_x(1, mostly_scalar)
-        first_hops(0, 2, 3, 4, 5)
+        first_hops(0, 0, 1, 2, 3)
         prepare_support(1, 0, (True, False))
-        first_hops(0, 6, 7)
+        first_hops(0, 4, 5)
         prepare_support(1, 1, (True, False))
+        first_hops(0, 6, 7)
         round_hop(0, 0)
         first_hops(1, 0, 1, 2, 3)
         turn_hop(0, 0)

@@ -66,26 +66,25 @@ def tile_adaptivegcn_pb_kernel(tc, x, support0, support1, out_0, out_1, out_2, o
 
         x_rows = x.rearrange("b c f -> (b c) f")
 
-        def load_x(r):
-            for g in range(PASSES):
-                cols = slice(g * K_PASS * STEPS, (g + 1) * K_PASS * STEPS)
-                nc.sync.dma_start(out=x_raw[r][:, cols], in_=x_rows[r * P : (r + 1) * P, cols])
+        def load(out, in_, pieces):
+            length = out.shape[1] // pieces
+            for start in range(0, out.shape[1], length):
+                cols = slice(start, start + length)
+                nc.sync.dma_start(out=out[:, cols], in_=in_[:, cols])
 
-        def load_support(s, pieces):
+        def load_x(r, pieces):
+            load(x_raw[r][:], x_rows[r * P : (r + 1) * P, :], pieces)
+
+        def load_support(s, half, pieces):
             blocks = supports[s].rearrange("(h p t) v -> h p (t v)", p=P, t=PACK)
-            length = PACK * NODES // pieces
-            for half in range(HALVES):
-                run = a_raw[s][:, half, :, :].rearrange("p t v -> p (t v)")
-                for start in range(0, PACK * NODES, length):
-                    nc.sync.dma_start(
-                        out=run[:, start : start + length],
-                        in_=blocks[half][:, start : start + length],
-                    )
+            load(a_raw[s][:, half, :, :].rearrange("p t v -> p (t v)"), blocks[half], pieces)
 
-        load_x(0)
-        load_support(0, 2)
-        load_x(1)
-        load_support(1, 1)
+        load_x(0, 2)
+        load_support(0, 0, 2)
+        load_support(0, 1, 1)
+        load_x(1, 1)
+        load_support(1, 0, 1)
+        load_support(1, 1, 1)
 
         def copy_out(on_vector, out, in_):
             if on_vector:
@@ -240,8 +239,7 @@ def tile_adaptivegcn_pb_kernel(tc, x, support0, support1, out_0, out_1, out_2, o
             for half in range(HALVES):
                 bank = multiply(hop_mx[s], tile, s, half)
                 copy_result(half == 0, result, half, bank)
-            last = s == 1 and tile >= ROWS // P - PAIR
-            store(second_out[s], tile, open_pair[0], together=not last)
+            store(second_out[s], tile, open_pair[0], together=(s == 0))
 
         def first_hops(s, *tiles):
             for tile in tiles:

@@ -35,7 +35,8 @@ def tile_adaptivegcn_pb_kernel(tc, x, support0, support1, out_0, out_1, out_2, o
         keep = ctx.enter_context(tc.tile_pool(name="keep", bufs=1))
         group_pool = ctx.enter_context(tc.tile_pool(name="group", bufs=4))
         sorted_pool = ctx.enter_context(tc.tile_pool(name="sorted", bufs=2))
-        result_pool = ctx.enter_context(tc.tile_pool(name="result", bufs=14))
+        words_pool = ctx.enter_context(tc.tile_pool(name="words", bufs=4))
+        result_pool = ctx.enter_context(tc.tile_pool(name="result", bufs=12))
         pair_pool = ctx.enter_context(tc.tile_pool(name="pair", bufs=8))
         banks = ctx.enter_context(tc.psum_pool(name="banks", bufs=8))
 
@@ -81,10 +82,10 @@ def tile_adaptivegcn_pb_kernel(tc, x, support0, support1, out_0, out_1, out_2, o
 
         load_x(0, 2)
         load_support(0, 0, 2)
-        load_support(0, 1, 1)
-        load_x(1, 1)
-        load_support(1, 0, 1)
-        load_support(1, 1, 1)
+        load_support(0, 1, 2)
+        load_x(1, 2)
+        load_support(1, 0, 2)
+        load_support(1, 1, 2)
 
         def copy_out(on_vector, out, in_):
             if on_vector:
@@ -99,64 +100,96 @@ def tile_adaptivegcn_pb_kernel(tc, x, support0, support1, out_0, out_1, out_2, o
                 bank[:].rearrange("m (t p) -> m p t", t=PACK),
             )
 
-        def prepare_x(r, on_vector):
+        VECTOR, SCALAR = True, False
+        held = {}
+
+        x_grouped = {}
+
+        def turn_x(r, h, g):
             words = x_raw[r][:].bitcast(F32)
-            grouped = sorted_pool.tile(
-                [P, 2 * PAIR, PASSES, STEPS, CHANNELS // PAIR, PACK], BF16, tag="sorted", align_bytes=64
+            bank = banks.tile([P, PACK, P], F32, tag="bank")
+            for t in range(PACK):
+                start = 2 * (g * K_PASS + t) + h
+                stop = start + 2 * PACK * (P - 1) + 1
+                nc.tensor.transpose(bank[:, t, :], words[:, start : stop : 2 * PACK], sorting[:])
+            held["x", r, h, g] = bank
+
+        def copy_x(r, h, g, on_vector):
+            if r not in x_grouped:
+                x_grouped[r] = sorted_pool.tile(
+                    [P, 2 * PAIR, PASSES, STEPS, CHANNELS // PAIR, PACK], BF16, tag="sorted", align_bytes=64, name="sorted"
+                )
+            values = held["x", r, h, g][:].rearrange("p t i -> p (t i)").bitcast(BF16)
+            copy_out(
+                on_vector,
+                x_grouped[r][:, :, g, 2 * h : 2 * h + 2, :, :],
+                values.rearrange("p (t a c o) -> p a o c t", t=PACK, a=2 * PAIR, o=2),
             )
-            for h in range(STEPS // 2):
-                for g in range(PASSES):
-                    bank = banks.tile([P, PACK, P], F32, tag="bank")
-                    for t in range(PACK):
-                        start = 2 * (g * K_PASS + t) + h
-                        stop = start + 2 * PACK * (P - 1) + 1
-                        nc.tensor.transpose(
-                            bank[:, t, :], words[:, start : stop : 2 * PACK], sorting[:]
-                        )
-                    values = bank[:].rearrange("p t i -> p (t i)").bitcast(BF16)
-                    copy_out(
-                        on_vector[h][g],
-                        grouped[:, :, g, 2 * h : 2 * h + 2, :, :],
-                        values.rearrange("p (t a c o) -> p a o c t", t=PACK, a=2 * PAIR, o=2),
-                    )
-            for b in range(2):
-                tiles = slice(TILES * r + PAIR * b, TILES * r + PAIR * (b + 1))
-                nc.vector.quantize_mx(
-                    out=x_mx[0][:, tiles, :, :].rearrange("p a g m -> p (a g m)").bitcast(FP8X4),
-                    scales=x_mx[1][:, tiles, :, :].rearrange("p a g m -> p (a g m)"),
-                    in_=grouped[:, PAIR * b : PAIR * (b + 1), :, :, :, :].rearrange(
-                        "p a g l c t -> p (a g l c t)"
-                    ),
-                )
 
-        def prepare_support(s, half, on_vector):
-            for g in range(PASSES):
-                grouped = group_pool.tile([P, WIDE, PACK], BF16, tag="grouped", align_bytes=64)
-                grouped_words = grouped[:].bitcast(F32)
-                for jj in range(2):
-                    bank = banks.tile([P, 2, PAIR, P], F32, tag="bank")
-                    for a in range(2):
-                        words = a_raw[s][:, half, 2 * jj + a, :].bitcast(F32)
-                        for u in range(PAIR):
-                            start = PAIR * g * P + u
-                            stop = start + PAIR * (P - 1) + 1
-                            nc.tensor.transpose(
-                                bank[:, a, u, :], words[:, start : stop : PAIR], identity[:]
-                            )
-                    copy_out(
-                        on_vector[jj],
-                        grouped_words[:, jj * 2 * P : (jj + 1) * 2 * P, :].rearrange(
-                            "p (a c) u -> p a c u", a=2
-                        ),
-                        bank[:].rearrange("p a u c -> p a c u"),
-                    )
-                nc.vector.quantize_mx(
-                    out=a_mx[s][0][:, half, g, :].bitcast(FP8X4),
-                    scales=a_mx[s][1][:, half, g, :],
-                    in_=grouped[:].rearrange("p c t -> p (c t)"),
-                )
+        def quantise_x(r, b):
+            tiles = slice(TILES * r + PAIR * b, TILES * r + PAIR * (b + 1))
+            nc.vector.quantize_mx(
+                out=x_mx[0][:, tiles, :, :].rearrange("p a g m -> p (a g m)").bitcast(FP8X4),
+                scales=x_mx[1][:, tiles, :, :].rearrange("p a g m -> p (a g m)"),
+                in_=x_grouped[r][:, PAIR * b : PAIR * (b + 1), :, :, :, :].rearrange("p a g l c t -> p (a g l c t)"),
+            )
 
-        def multiply(rows_mx, tile, s, half):
+        words_sorted = {}
+        a_grouped = {}
+
+        def sort_words(s, half, jj):
+            words = words_pool.tile([P, 2, PASSES, PAIR, P], F32, tag="words", name="words")
+            nc.vector.tensor_copy(
+                out=words[:],
+                in_=a_raw[s][:, half, 2 * jj : 2 * jj + 2, :].bitcast(F32).rearrange(
+                    "p a (g q u) -> p a g u q", g=PASSES, u=PAIR
+                ),
+            )
+            words_sorted[s, half, jj] = words
+
+        def turn_support(s, half, g, jj):
+            bank = banks.tile([P, 2, PAIR, P], F32, tag="bank")
+            for a in range(2):
+                words = a_raw[s][:, half, 2 * jj + a, :].bitcast(F32)
+                for u in range(PAIR):
+                    start = PAIR * g * P + u
+                    stop = start + PAIR * (P - 1) + 1
+                    nc.tensor.transpose(
+                        bank[:, a, u, :],
+                        words_sorted[s, half, jj][:, a, g, u, :]
+                        if (s, half, jj) in words_sorted
+                        else words[:, start : stop : PAIR],
+                        identity[:],
+                    )
+            held["a", s, half, g, jj] = bank
+
+        def copy_support(s, half, g, jj, on_vector):
+            if (s, half, g) not in a_grouped:
+                a_grouped[s, half, g] = group_pool.tile(
+                    [P, WIDE, PACK], BF16, tag="grouped", align_bytes=64, name="grouped"
+                )
+            copy_out(
+                on_vector,
+                a_grouped[s, half, g][:].bitcast(F32)[:, jj * 2 * P : (jj + 1) * 2 * P, :].rearrange(
+                    "p (a c) u -> p a c u", a=2
+                ),
+                held["a", s, half, g, jj][:].rearrange("p a u c -> p a c u"),
+            )
+
+        def quantise_support(s, half, g):
+            nc.vector.quantize_mx(
+                out=a_mx[s][0][:, half, g, :].bitcast(FP8X4),
+                scales=a_mx[s][1][:, half, g, :],
+                in_=a_grouped[s, half, g][:].rearrange("p c t -> p (c t)"),
+            )
+
+        results = {}
+        pairs = {}
+        rounded = {}
+        hop_grouped = {}
+
+        def multiply(hop, s, tile, half):
+            rows_mx = x_mx if hop == 1 else hop_mx[s]
             bank = banks.tile([P, WIDE], F32, tag="bank")
             for g in range(PASSES):
                 nc.tensor.matmul_mx(
@@ -168,27 +201,17 @@ def tile_adaptivegcn_pb_kernel(tc, x, support0, support1, out_0, out_1, out_2, o
                     start=(g == 0),
                     stop=(g == PASSES - 1),
                 )
-            return bank
+            held[hop, s, tile, half] = bank
 
-        rounded = {}
-        results = {}
+        def copy_product(hop, s, tile, half, on_vector):
+            if (hop, s, tile // PAIR) not in pairs:
+                pairs[hop, s, tile // PAIR] = pair_pool.tile([P, PAIR, NODES], F32, tag="pair", name="pair")
+            result = pairs[hop, s, tile // PAIR][:, tile % PAIR, :]
+            copy_result(on_vector, result, half, held[hop, s, tile, half])
 
-        def round_hop(s, r):
-            for tile in range(TILES * r, TILES * (r + 1)):
-                result = results[s, tile]
-                low = result_pool.tile([P, NODES], BF16, tag="rounded")
-                nc.vector.tensor_copy(
-                    out=low[:].rearrange("m (g u q e) -> m g u q e", g=PASSES, u=PAIR, e=PAIR),
-                    in_=result.rearrange("m (g q u e) -> m g u q e", g=PASSES, u=PAIR, e=PAIR),
-                )
-                rounded[s, tile] = low
-
-        def open_result(tile, open_pairs):
-            if tile % PAIR == 0:
-                open_pairs[0] = pair_pool.tile([P, PAIR, NODES], F32, tag="pair", name="pair")
-            return open_pairs[0][:, tile % PAIR, :]
-
-        def store(out, tile, pair, together):
+        def store(hop, s, tile, together):
+            out = (first_out if hop == 1 else second_out)[s]
+            pair = pairs[hop, s, tile // PAIR]
             rows = out[tile // PAIR * PAIR * P : (tile // PAIR + 1) * PAIR * P, :]
             if not together:
                 nc.sync.dma_start(
@@ -201,74 +224,150 @@ def tile_adaptivegcn_pb_kernel(tc, x, support0, support1, out_0, out_1, out_2, o
                     in_=pair[:].rearrange("p a w -> p (a w)"),
                 )
 
-        open_pair = [None]
+        def round_hop(s, tile):
+            low = result_pool.tile([P, NODES], BF16, tag="rounded", name="rounded_tile")
+            nc.vector.tensor_copy(
+                out=low[:].rearrange("m (g u q e) -> m g u q e", g=PASSES, u=PAIR, e=PAIR),
+                in_=pairs[1, s, tile // PAIR][:, tile % PAIR, :].rearrange(
+                    "m (g q u e) -> m g u q e", g=PASSES, u=PAIR, e=PAIR
+                ),
+            )
+            rounded[s, tile] = low
 
-        def first_hop(s, tile):
-            result = open_result(tile, open_pair)
-            for half in range(HALVES):
-                bank = multiply(x_mx, tile, s, half)
-                copy_result(False, result, half, bank)
-            store(first_out[s], tile, open_pair[0], together=(s == 1))
-            results[s, tile] = result
+        def turn_hop(s, tile):
+            words = rounded[s, tile][:].bitcast(F32)
+            bank = banks.tile([P, PASSES, PAIR, P], F32, tag="bank")
+            for g in range(PASSES):
+                for u in range(PAIR):
+                    start = (PAIR * g + u) * P
+                    nc.tensor.transpose(bank[:, g, u, :], words[:, start : start + P], identity[:])
+            held["hop", s, tile] = bank
 
-        def turn_hop(s, r):
-            for first in range(TILES * r, TILES * (r + 1), 2):
-                grouped = group_pool.tile([P, 2, PASSES, P, PACK], BF16, tag="grouped", align_bytes=64)
-                for a in range(2):
-                    words = rounded[s, first + a][:].bitcast(F32)
-                    bank = banks.tile([P, PASSES, PAIR, P], F32, tag="bank")
-                    for g in range(PASSES):
-                        for u in range(PAIR):
-                            start = (PAIR * g + u) * P
-                            nc.tensor.transpose(bank[:, g, u, :], words[:, start : start + P], identity[:])
-                    copy_out(
-                        a == 0,
-                        grouped[:, a, :, :, :].rearrange("p g c t -> p g (c t)").bitcast(F32).rearrange(
-                            "p g (c u) -> p g c u", u=PAIR
-                        ),
-                        bank[:].rearrange("p g u c -> p g c u"),
-                    )
-                nc.vector.quantize_mx(
-                    out=hop_mx[s][0][:, first : first + 2, :, :].rearrange("p a g m -> p (a g m)").bitcast(FP8X4),
-                    scales=hop_mx[s][1][:, first : first + 2, :, :].rearrange("p a g m -> p (a g m)"),
-                    in_=grouped[:].rearrange("p a g m t -> p (a g m t)"),
+        def copy_hop(s, tile, on_vector):
+            if (s, tile // 2) not in hop_grouped:
+                hop_grouped[s, tile // 2] = group_pool.tile(
+                    [P, 2, PASSES, P, PACK], BF16, tag="grouped", align_bytes=64, name="grouped"
                 )
+            copy_out(
+                on_vector,
+                hop_grouped[s, tile // 2][:, tile % 2, :, :, :]
+                .rearrange("p g c t -> p g (c t)")
+                .bitcast(F32)
+                .rearrange("p g (c u) -> p g c u", u=PAIR),
+                held["hop", s, tile][:].rearrange("p g u c -> p g c u"),
+            )
+
+        def quantise_hop(s, first):
+            nc.vector.quantize_mx(
+                out=hop_mx[s][0][:, first : first + 2, :, :].rearrange("p a g m -> p (a g m)").bitcast(FP8X4),
+                scales=hop_mx[s][1][:, first : first + 2, :, :].rearrange("p a g m -> p (a g m)"),
+                in_=hop_grouped[s, first // 2][:].rearrange("p a g m t -> p (a g m t)"),
+            )
+
+        ctx.enter_context(tc.manual_schedule())
+
+        for g in range(PASSES):
+            for h in range(2):
+                turn_x(0, h, g)
+                copy_x(0, h, g, SCALAR if h == 0 else VECTOR)
+        quantise_x(0, 0)
+        for jj in range(2):
+            for g in range(PASSES):
+                turn_support(0, 0, g, jj)
+                copy_support(0, 0, g, jj, SCALAR)
+        sort_words(0, 1, 0)
+        quantise_support(0, 0, 0)
+        quantise_support(0, 0, 1)
+        quantise_x(0, 1)
+        sort_words(0, 1, 1)
+
+        def later_support(s, half, jj, vector_g):
+            for g in range(PASSES):
+                turn_support(s, half, g, jj)
+                copy_support(s, half, g, jj, VECTOR if g == vector_g else SCALAR)
+
+        def first_product(s, tile, half):
+            multiply(1, s, tile, half)
+
+        def first_result(s, tile, half, on_vector=SCALAR):
+            copy_product(1, s, tile, half, on_vector)
+            if half == HALVES - 1:
+                store(1, s, tile, together=(s == 1))
+
+        def first_hop(s, tile, vector_half=None):
+            for half in range(HALVES):
+                first_product(s, tile, half)
+                first_result(s, tile, half, VECTOR if half == vector_half else SCALAR)
+
+        later_support(0, 1, 0, None)
+        for tile in range(TILES):
+            first_product(0, tile, 0)
+        for tile in range(TILES):
+            first_result(0, tile, 0)
+        later_support(0, 1, 1, None)
+
+        def later_x(g):
+            for h in range(2):
+                turn_x(1, h, g)
+                copy_x(1, h, g, VECTOR if h == 0 else SCALAR)
+
+        later_x(0)
+        quantise_support(0, 1, 0)
+        quantise_support(0, 1, 1)
+        later_x(1)
+        quantise_x(1, 0)
+        quantise_x(1, 1)
+        for tile in range(TILES):
+            first_product(0, tile, 1)
+            first_result(0, tile, 1)
+        sort_words(1, 0, 0)
+        sort_words(1, 0, 1)
+        first_hop(0, 4)
+        later_support(1, 0, 0, 0)
+        later_support(1, 0, 1, 0)
+        sort_words(1, 1, 0)
+        quantise_support(1, 0, 0)
+        sort_words(1, 1, 1)
+        quantise_support(1, 0, 1)
+        first_hop(0, 5)
+        first_hop(0, 6)
+        later_support(1, 1, 0, 0)
+        later_support(1, 1, 1, 0)
+        quantise_support(1, 1, 0)
+        quantise_support(1, 1, 1)
+        first_hop(0, 7)
+
+        def turn_tiles(s, r):
+            tiles = range(TILES * r, TILES * (r + 1))
+            for tile in tiles:
+                turn_hop(s, tile)
+                copy_hop(s, tile, VECTOR if tile % 2 == 0 else SCALAR)
+            for first in tiles[::2]:
+                quantise_hop(s, first)
 
         def second_hop(s, tile):
-            result = open_result(tile, open_pair)
             for half in range(HALVES):
-                bank = multiply(hop_mx[s], tile, s, half)
-                copy_result(half == 0, result, half, bank)
-            store(second_out[s], tile, open_pair[0], together=(s == 0))
+                multiply(2, s, tile, half)
+                copy_product(2, s, tile, half, VECTOR if half == 0 else SCALAR)
+            store(2, s, tile, together=(s == 0))
 
-        def first_hops(s, *tiles):
-            for tile in tiles:
-                first_hop(s, tile)
-
-        def second_hops(s, *tiles):
-            for tile in tiles:
-                second_hop(s, tile)
-
-        mostly_scalar = ((False, True), (False, True))
-        prepare_x(0, mostly_scalar)
-        prepare_support(0, 0, (False, False))
-        prepare_support(0, 1, (False, False))
-        prepare_x(1, mostly_scalar)
-        first_hops(0, 0, 1, 2, 3)
-        prepare_support(1, 0, (True, False))
-        first_hops(0, 4, 5)
-        prepare_support(1, 1, (True, False))
-        first_hops(0, 6, 7)
-        round_hop(0, 0)
-        first_hops(1, 0, 1, 2, 3)
-        turn_hop(0, 0)
-        round_hop(0, 1)
-        first_hops(1, 4, 5, 6, 7)
-        turn_hop(0, 1)
-        round_hop(1, 0)
-        second_hops(0, 0, 1, 2, 3)
-        turn_hop(1, 0)
-        round_hop(1, 1)
-        second_hops(0, 4, 5, 6, 7)
-        turn_hop(1, 1)
-        second_hops(1, 0, 1, 2, 3, 4, 5, 6, 7)
+        for tile in range(TILES):
+            round_hop(0, tile)
+            round_hop(0, TILES + tile)
+            first_hop(1, tile, vector_half=0 if tile == TILES - 1 else None)
+        turn_tiles(0, 0)
+        for tile in range(TILES):
+            round_hop(1, tile)
+            first_hop(1, TILES + tile, vector_half=0 if tile == TILES - 1 else None)
+        turn_tiles(0, 1)
+        for tile in range(TILES):
+            second_hop(0, tile)
+            round_hop(1, TILES + tile)
+        turn_tiles(1, 0)
+        for tile in range(TILES, 2 * TILES):
+            second_hop(0, tile)
+        for tile in range(2):
+            second_hop(1, tile)
+        turn_tiles(1, 1)
+        for tile in range(2, 2 * TILES):
+            second_hop(1, tile)

@@ -266,28 +266,21 @@ def tile_adaptivegcn_pb_kernel(tc, x, support0, support1, out_0, out_1, out_2, o
 
         ctx.enter_context(tc.manual_schedule())
 
-        for g in range(PASSES):
-            for h in range(2):
-                turn_x(0, h, g)
-                copy_x(0, h, g, SCALAR if h == 0 else VECTOR)
-        quantise_x(0, 0)
-        for jj in range(2):
+        def prepare_x(r, scalar_h):
             for g in range(PASSES):
-                turn_support(0, 0, g, jj)
-                copy_support(0, 0, g, jj, SCALAR)
-        sort_words(0, 1, 0)
-        quantise_support(0, 0, 0)
-        quantise_support(0, 0, 1)
-        quantise_x(0, 1)
-        sort_words(0, 1, 1)
+                for h in range(2):
+                    turn_x(r, h, g)
+                    copy_x(r, h, g, SCALAR if h == scalar_h else VECTOR)
 
-        def later_support(s, half, jj, vector_g):
+        def prepare_support(s, half, vector_banks):
+            for jj in range(2):
+                for g in range(PASSES):
+                    turn_support(s, half, g, jj)
+                    copy_support(s, half, g, jj, VECTOR if (jj, g) in vector_banks else SCALAR)
+
+        def quantise_half(s, half):
             for g in range(PASSES):
-                turn_support(s, half, g, jj)
-                copy_support(s, half, g, jj, VECTOR if g == vector_g else SCALAR)
-
-        def first_product(s, tile, half):
-            multiply(1, s, tile, half)
+                quantise_support(s, half, g)
 
         def first_result(s, tile, half, on_vector=SCALAR):
             copy_product(1, s, tile, half, on_vector)
@@ -296,46 +289,43 @@ def tile_adaptivegcn_pb_kernel(tc, x, support0, support1, out_0, out_1, out_2, o
 
         def first_hop(s, tile, vector_half=None):
             for half in range(HALVES):
-                first_product(s, tile, half)
+                multiply(1, s, tile, half)
                 first_result(s, tile, half, VECTOR if half == vector_half else SCALAR)
 
-        later_support(0, 1, 0, None)
-        for tile in range(TILES):
-            first_product(0, tile, 0)
-        for tile in range(TILES):
-            first_result(0, tile, 0)
-        later_support(0, 1, 1, None)
-
-        def later_x(g):
+        prepare_x(0, scalar_h=0)
+        quantise_x(0, 0)
+        quantise_x(0, 1)
+        prepare_support(0, 0, ())
+        quantise_half(0, 0)
+        prepare_support(0, 1, ((0, 1),))
+        for g in range(PASSES):
             for h in range(2):
                 turn_x(1, h, g)
-                copy_x(1, h, g, VECTOR if h == 0 else SCALAR)
-
-        later_x(0)
-        quantise_support(0, 1, 0)
-        quantise_support(0, 1, 1)
-        later_x(1)
+                copy_x(1, h, g, SCALAR if h == 1 else VECTOR)
+            if g == 0:
+                quantise_half(0, 1)
+        for tile in range(TILES):
+            multiply(1, 0, tile, 0)
+        for tile in range(TILES):
+            first_result(0, tile, 0)
         quantise_x(1, 0)
         quantise_x(1, 1)
-        for tile in range(TILES):
-            first_product(0, tile, 1)
-            first_result(0, tile, 1)
         sort_words(1, 0, 0)
         sort_words(1, 0, 1)
-        first_hop(0, 4)
-        later_support(1, 0, 0, 0)
-        later_support(1, 0, 1, 0)
+        for tile in range(TILES):
+            multiply(1, 0, tile, 1)
+            first_result(0, tile, 1)
+        prepare_support(1, 0, ((0, 0), (1, 0)))
         sort_words(1, 1, 0)
         quantise_support(1, 0, 0)
         sort_words(1, 1, 1)
         quantise_support(1, 0, 1)
+        first_hop(0, 4)
         first_hop(0, 5)
+        prepare_support(1, 1, ((0, 0), (1, 0)))
+        quantise_half(1, 1)
         first_hop(0, 6)
-        later_support(1, 1, 0, 0)
-        later_support(1, 1, 1, 0)
-        quantise_support(1, 1, 0)
-        quantise_support(1, 1, 1)
-        first_hop(0, 7)
+        first_hop(0, 7, vector_half=0)
 
         def turn_tiles(s, r):
             tiles = range(TILES * r, TILES * (r + 1))
@@ -349,16 +339,16 @@ def tile_adaptivegcn_pb_kernel(tc, x, support0, support1, out_0, out_1, out_2, o
             for half in range(HALVES):
                 multiply(2, s, tile, half)
                 copy_product(2, s, tile, half, VECTOR if half == 0 else SCALAR)
-            store(2, s, tile, together=(s == 0))
+            store(2, s, tile, together=False)
 
         for tile in range(TILES):
-            round_hop(0, tile)
-            round_hop(0, TILES + tile)
+            round_hop(0, 2 * tile)
+            round_hop(0, 2 * tile + 1)
             first_hop(1, tile, vector_half=0 if tile == TILES - 1 else None)
         turn_tiles(0, 0)
         for tile in range(TILES):
             round_hop(1, tile)
-            first_hop(1, TILES + tile, vector_half=0 if tile == TILES - 1 else None)
+            first_hop(1, TILES + tile)
         turn_tiles(0, 1)
         for tile in range(TILES):
             second_hop(0, tile)

@@ -114,6 +114,32 @@ def tile_adaptivegcn_pb_kernel(tc, x, support0, support1, out_0, out_1, out_2, o
                 nc.tensor.transpose(bank[:, t, :], words[:, start : stop : 2 * PACK], sorting[:])
             held["x", r, h, g] = bank
 
+        def sort_x(g):
+            nc.vector.tensor_copy(
+                out=x_raw[0][:].rearrange("p (g l u q e) -> p g l u q e", g=PASSES, l=STEPS, u=PAIR, e=PAIR)[:, g],
+                in_=x_raw[1][:].rearrange("p (g q u e l) -> p g l u q e", g=PASSES, u=PAIR, e=PAIR, l=STEPS)[:, g],
+            )
+
+        def turn_sorted_x(h, g):
+            words = x_raw[0][:].bitcast(F32)
+            bank = banks.tile([P, PAIR, PAIR, P], F32, tag="bank")
+            for o in range(PAIR):
+                for u in range(PAIR):
+                    start = ((g * STEPS + 2 * h + o) * PAIR + u) * P
+                    nc.tensor.transpose(bank[:, o, u, :], words[:, start : start + P], sorting[:])
+            held["x", 1, h, g] = bank
+
+        def copy_sorted_x(h, g, on_vector):
+            if 1 not in x_grouped:
+                x_grouped[1] = sorted_pool.tile(
+                    [P, 2 * PAIR, PASSES, STEPS, CHANNELS // PAIR, PACK], BF16, tag="sorted", align_bytes=64, name="sorted"
+                )
+            copy_out(
+                on_vector,
+                x_grouped[1][:].bitcast(F32)[:, :, g, 2 * h : 2 * h + 2, :, :],
+                held["x", 1, h, g][:].rearrange("p o u (a c) -> p a o c u", a=2 * PAIR),
+            )
+
         def copy_x(r, h, g, on_vector):
             if r not in x_grouped:
                 x_grouped[r] = sorted_pool.tile(
@@ -298,34 +324,36 @@ def tile_adaptivegcn_pb_kernel(tc, x, support0, support1, out_0, out_1, out_2, o
         prepare_support(0, 0, ())
         quantise_half(0, 0)
         prepare_support(0, 1, ((0, 1),))
+        quantise_half(0, 1)
         for g in range(PASSES):
-            for h in range(2):
-                turn_x(1, h, g)
-                copy_x(1, h, g, SCALAR if h == 1 else VECTOR)
-            if g == 0:
-                quantise_half(0, 1)
+            sort_x(g)
+            sort_words(1, 0, g)
         for tile in range(TILES):
             multiply(1, 0, tile, 0)
         for tile in range(TILES):
             first_result(0, tile, 0)
-        quantise_x(1, 0)
-        quantise_x(1, 1)
-        sort_words(1, 0, 0)
-        sort_words(1, 0, 1)
         for tile in range(TILES):
             multiply(1, 0, tile, 1)
+        for tile in range(2):
             first_result(0, tile, 1)
-        prepare_support(1, 0, ((0, 0), (1, 0)))
+        for g in range(PASSES):
+            for h in range(2):
+                turn_sorted_x(h, g)
+                copy_sorted_x(h, g, SCALAR if h == 0 else VECTOR)
+        for tile in range(2, TILES):
+            first_result(0, tile, 1)
+        quantise_x(1, 0)
         sort_words(1, 1, 0)
-        quantise_support(1, 0, 0)
         sort_words(1, 1, 1)
-        quantise_support(1, 0, 1)
+        prepare_support(1, 0, ((0, 0), (1, 0)))
+        quantise_x(1, 1)
+        quantise_half(1, 0)
         first_hop(0, 4)
         first_hop(0, 5)
         prepare_support(1, 1, ((0, 0), (1, 0)))
         quantise_half(1, 1)
         first_hop(0, 6)
-        first_hop(0, 7, vector_half=0)
+        first_hop(0, 7)
 
         def turn_tiles(s, r):
             tiles = range(TILES * r, TILES * (r + 1))
@@ -344,7 +372,7 @@ def tile_adaptivegcn_pb_kernel(tc, x, support0, support1, out_0, out_1, out_2, o
         for tile in range(TILES):
             round_hop(0, 2 * tile)
             round_hop(0, 2 * tile + 1)
-            first_hop(1, tile, vector_half=0 if tile == TILES - 1 else None)
+            first_hop(1, tile)
         turn_tiles(0, 0)
         for tile in range(TILES):
             round_hop(1, tile)
@@ -356,8 +384,8 @@ def tile_adaptivegcn_pb_kernel(tc, x, support0, support1, out_0, out_1, out_2, o
         turn_tiles(1, 0)
         for tile in range(TILES, 2 * TILES):
             second_hop(0, tile)
-        for tile in range(2):
+        for tile in range(3):
             second_hop(1, tile)
         turn_tiles(1, 1)
-        for tile in range(2, 2 * TILES):
+        for tile in range(3, 2 * TILES):
             second_hop(1, tile)

@@ -324,29 +324,27 @@ def tile_adaptivegcn_pb_kernel(tc, x, support0, support1, out_0, out_1, out_2, o
         prepare_support(0, 0, ())
         quantise_half(0, 0)
         prepare_support(0, 1, ((0, 1),))
-        quantise_half(0, 1)
         for g in range(PASSES):
             sort_x(g)
-            sort_words(1, 0, g)
+        quantise_half(0, 1)
         for tile in range(TILES):
             multiply(1, 0, tile, 0)
         for tile in range(TILES):
             first_result(0, tile, 0)
-        for tile in range(TILES):
-            multiply(1, 0, tile, 1)
-        for tile in range(2):
-            first_result(0, tile, 1)
         for g in range(PASSES):
             for h in range(2):
                 turn_sorted_x(h, g)
-                copy_sorted_x(h, g, SCALAR if h == 0 else VECTOR)
-        for tile in range(2, TILES):
-            first_result(0, tile, 1)
+                copy_sorted_x(h, g, SCALAR if h == 1 else VECTOR)
+        sort_words(1, 0, 0)
+        sort_words(1, 0, 1)
         quantise_x(1, 0)
+        for tile in range(TILES):
+            multiply(1, 0, tile, 1)
+            first_result(0, tile, 1)
+        quantise_x(1, 1)
         sort_words(1, 1, 0)
         sort_words(1, 1, 1)
         prepare_support(1, 0, ((0, 0), (1, 0)))
-        quantise_x(1, 1)
         quantise_half(1, 0)
         first_hop(0, 4)
         first_hop(0, 5)
@@ -384,8 +382,8 @@ def tile_adaptivegcn_pb_kernel(tc, x, support0, support1, out_0, out_1, out_2, o
         turn_tiles(1, 0)
         for tile in range(TILES, 2 * TILES):
             second_hop(0, tile)
-        for tile in range(3):
+        for tile in range(2):
             second_hop(1, tile)
         turn_tiles(1, 1)
-        for tile in range(3, 2 * TILES):
+        for tile in range(2, 2 * TILES):
             second_hop(1, tile)

from contextlib import ExitStack

import concourse.mybir as mybir
from concourse.masks import make_identity

F32 = mybir.dt.float32
BF16 = mybir.dt.bfloat16
U32 = mybir.dt.uint32
U8 = mybir.dt.uint8
FP8X4 = mybir.dt.float8_e4m3fn_x4

P = 128
PACK = 4
PAIR = 2
K_PASS = P * PACK
NODES = 1024
ROWS = 1024
STEPS = 4
CHANNELS = 64
PASSES = NODES // K_PASS
WIDE = 512
HALVES = ROWS // WIDE
TILES = WIDE // P

FLOPS = 4 * 2 * ROWS * NODES * NODES


def tile_adaptivegcn_pb_kernel(tc, x, support0, support1, out_0, out_1, out_2, out_3):
    nc = tc.nc
    supports = (support0, support1)
    first_out = [o.rearrange("n c w -> (n c) w") for o in (out_0, out_2)]
    second_out = [o.rearrange("n c w -> (n c) w") for o in (out_1, out_3)]

    with ExitStack() as ctx:
        keep = ctx.enter_context(tc.tile_pool(name="keep", bufs=1))
        group_pool = ctx.enter_context(tc.tile_pool(name="group", bufs=4))
        sorted_pool = ctx.enter_context(tc.tile_pool(name="sorted", bufs=2))
        words_pool = ctx.enter_context(tc.tile_pool(name="words", bufs=4))
        result_pool = ctx.enter_context(tc.tile_pool(name="result", bufs=12))
        pair_pool = ctx.enter_context(tc.tile_pool(name="pair", bufs=8))
        banks = ctx.enter_context(tc.psum_pool(name="banks", bufs=8))

        identity = keep.tile([P, P], F32, name="identity")
        make_identity(nc, identity[:])
        sorting = keep.tile([P, P], F32, name="sorting")
        nc.vector.tensor_copy(
            out=sorting[:].rearrange("p (b a c) -> p b a c", b=2, a=PAIR),
            in_=identity[:].rearrange("p (b c a) -> p b a c", b=2, a=PAIR),
        )

        x_raw = [keep.tile([P, NODES * STEPS], BF16, name="x_raw%d" % r) for r in range(HALVES)]
        a_raw = [keep.tile([P, HALVES, PACK, NODES], BF16, name="a_raw%d" % s) for s in range(2)]

        def row_operand(name):
            codes = keep.tile([P, ROWS // P, PASSES, P], U32, name=name + "_codes", align_bytes=64)
            scales = keep.tile([P, ROWS // P, PASSES, P], U8, name=name + "_scales", align_bytes=64)
            return codes, scales

        def support_operand(name):
            codes = keep.tile([P, HALVES, PASSES, WIDE], U32, name=name + "_codes", align_bytes=64)
            scales = keep.tile([P, HALVES, PASSES, WIDE], U8, name=name + "_scales", align_bytes=64)
            return codes, scales

        x_mx = row_operand("x")
        a_mx = [support_operand("a%d" % s) for s in range(2)]
        hop_mx = [row_operand("hop%d" % s) for s in range(2)]

        x_rows = x.rearrange("b c f -> (b c) f")

        def load(out, in_, pieces):
            length = out.shape[1] // pieces
            for start in range(0, out.shape[1], length):
                cols = slice(start, start + length)
                nc.sync.dma_start(out=out[:, cols], in_=in_[:, cols])

        def load_x(r, pieces):
            load(x_raw[r][:], x_rows[r * P : (r + 1) * P, :], pieces)

        def load_support(s, half, pieces):
            blocks = supports[s].rearrange("(h p t) v -> h p (t v)", p=P, t=PACK)
            load(a_raw[s][:, half, :, :].rearrange("p t v -> p (t v)"), blocks[half], pieces)

        load_x(0, 2)
        load_support(0, 0, 2)
        load_support(0, 1, 2)
        load_x(1, 2)
        load_support(1, 0, 2)
        load_support(1, 1, 2)

        def copy_out(on_vector, out, in_):
            if on_vector:
                nc.vector.tensor_copy(out=out, in_=in_)
            else:
                nc.scalar.copy(out=out, in_=in_)

        def copy_result(on_vector, result, half, bank):
            copy_out(
                on_vector,
                result[:, half * WIDE : (half + 1) * WIDE].rearrange("m (p t) -> m p t", t=PACK),
                bank[:].rearrange("m (t p) -> m p t", t=PACK),
            )

        VECTOR, SCALAR = True, False
        held = {}

        x_grouped = {}

        def turn_x(r, h, g):
            words = x_raw[r][:].bitcast(F32)
            bank = banks.tile([P, PACK, P], F32, tag="bank")
            for t in range(PACK):
                start = 2 * (g * K_PASS + t) + h
                stop = start + 2 * PACK * (P - 1) + 1
                nc.tensor.transpose(bank[:, t, :], words[:, start : stop : 2 * PACK], sorting[:])
            held["x", r, h, g] = bank

        def sort_x(g):
            nc.vector.tensor_copy(
                out=x_raw[0][:].rearrange("p (g l u q e) -> p g l u q e", g=PASSES, l=STEPS, u=PAIR, e=PAIR)[:, g],
                in_=x_raw[1][:].rearrange("p (g q u e l) -> p g l u q e", g=PASSES, u=PAIR, e=PAIR, l=STEPS)[:, g],
            )

        def turn_sorted_x(h, g):
            words = x_raw[0][:].bitcast(F32)
            bank = banks.tile([P, PAIR, PAIR, P], F32, tag="bank")
            for o in range(PAIR):
                for u in range(PAIR):
                    start = ((g * STEPS + 2 * h + o) * PAIR + u) * P
                    nc.tensor.transpose(bank[:, o, u, :], words[:, start : start + P], sorting[:])
            held["x", 1, h, g] = bank

        def copy_sorted_x(h, g, on_vector):
            if 1 not in x_grouped:
                x_grouped[1] = sorted_pool.tile(
                    [P, 2 * PAIR, PASSES, STEPS, CHANNELS // PAIR, PACK], BF16, tag="sorted", align_bytes=64, name="sorted"
                )
            copy_out(
                on_vector,
                x_grouped[1][:].bitcast(F32)[:, :, g, 2 * h : 2 * h + 2, :, :],
                held["x", 1, h, g][:].rearrange("p o u (a c) -> p a o c u", a=2 * PAIR),
            )

        def copy_x(r, h, g, on_vector):
            if r not in x_grouped:
                x_grouped[r] = sorted_pool.tile(
                    [P, 2 * PAIR, PASSES, STEPS, CHANNELS // PAIR, PACK], BF16, tag="sorted", align_bytes=64, name="sorted"
                )
            values = held["x", r, h, g][:].rearrange("p t i -> p (t i)").bitcast(BF16)
            copy_out(
                on_vector,
                x_grouped[r][:, :, g, 2 * h : 2 * h + 2, :, :],
                values.rearrange("p (t a c o) -> p a o c t", t=PACK, a=2 * PAIR, o=2),
            )

        def quantise_x(r, b):
            tiles = slice(TILES * r + PAIR * b, TILES * r + PAIR * (b + 1))
            nc.vector.quantize_mx(
                out=x_mx[0][:, tiles, :, :].rearrange("p a g m -> p (a g m)").bitcast(FP8X4),
                scales=x_mx[1][:, tiles, :, :].rearrange("p a g m -> p (a g m)"),
                in_=x_grouped[r][:, PAIR * b : PAIR * (b + 1), :, :, :, :].rearrange("p a g l c t -> p (a g l c t)"),
            )

        words_sorted = {}
        a_grouped = {}

        def sort_words(s, half, jj):
            words = words_pool.tile([P, 2, PASSES, PAIR, P], F32, tag="words", name="words")
            nc.vector.tensor_copy(
                out=words[:],
                in_=a_raw[s][:, half, 2 * jj : 2 * jj + 2, :].bitcast(F32).rearrange(
                    "p a (g q u) -> p a g u q", g=PASSES, u=PAIR
                ),
            )
            words_sorted[s, half, jj] = words

        def turn_support(s, half, g, jj):
            bank = banks.tile([P, 2, PAIR, P], F32, tag="bank")
            for a in range(2):
                words = a_raw[s][:, half, 2 * jj + a, :].bitcast(F32)
                for u in range(PAIR):
                    start = PAIR * g * P + u
                    stop = start + PAIR * (P - 1) + 1
                    nc.tensor.transpose(
                        bank[:, a, u, :],
                        words_sorted[s, half, jj][:, a, g, u, :]
                        if (s, half, jj) in words_sorted
                        else words[:, start : stop : PAIR],
                        identity[:],
                    )
            held["a", s, half, g, jj] = bank

        def copy_support(s, half, g, jj, on_vector):
            if (s, half, g) not in a_grouped:
                a_grouped[s, half, g] = group_pool.tile(
                    [P, WIDE, PACK], BF16, tag="grouped", align_bytes=64, name="grouped"
                )
            copy_out(
                on_vector,
                a_grouped[s, half, g][:].bitcast(F32)[:, jj * 2 * P : (jj + 1) * 2 * P, :].rearrange(
                    "p (a c) u -> p a c u", a=2
                ),
                held["a", s, half, g, jj][:].rearrange("p a u c -> p a c u"),
            )

        def quantise_support(s, half, g):
            nc.vector.quantize_mx(
                out=a_mx[s][0][:, half, g, :].bitcast(FP8X4),
                scales=a_mx[s][1][:, half, g, :],
                in_=a_grouped[s, half, g][:].rearrange("p c t -> p (c t)"),
            )

        results = {}
        pairs = {}
        rounded = {}
        hop_grouped = {}

        def multiply(hop, s, tile, half):
            rows_mx = x_mx if hop == 1 else hop_mx[s]
            bank = banks.tile([P, WIDE], F32, tag="bank")
            for g in range(PASSES):
                nc.tensor.matmul_mx(
                    out=bank[:],
                    lhsT=rows_mx[0][:, tile, g, :].bitcast(FP8X4),
                    lhsT_scale=rows_mx[1][:, tile, g, :],
                    rhs=a_mx[s][0][:, half, g, :].bitcast(FP8X4),
                    rhs_scale=a_mx[s][1][:, half, g, :],
                    start=(g == 0),
                    stop=(g == PASSES - 1),
                )
            held[hop, s, tile, half] = bank

        def copy_product(hop, s, tile, half, on_vector):
            if (hop, s, tile // PAIR) not in pairs:
                pairs[hop, s, tile // PAIR] = pair_pool.tile([P, PAIR, NODES], F32, tag="pair", name="pair")
            result = pairs[hop, s, tile // PAIR][:, tile % PAIR, :]
            copy_result(on_vector, result, half, held[hop, s, tile, half])

        def store(hop, s, tile, together):
            out = (first_out if hop == 1 else second_out)[s]
            pair = pairs[hop, s, tile // PAIR]
            rows = out[tile // PAIR * PAIR * P : (tile // PAIR + 1) * PAIR * P, :]
            if not together:
                nc.sync.dma_start(
                    out=rows.rearrange("(m a) w -> m a w", a=PAIR)[:, tile % PAIR, :],
                    in_=pair[:, tile % PAIR, :],
                )
            elif tile % PAIR == PAIR - 1:
                nc.sync.dma_start(
                    out=rows.rearrange("(m a) w -> m (a w)", a=PAIR),
                    in_=pair[:].rearrange("p a w -> p (a w)"),
                )

        def round_hop(s, tile):
            low = result_pool.tile([P, NODES], BF16, tag="rounded", name="rounded_tile")
            nc.vector.tensor_copy(
                out=low[:].rearrange("m (g u q e) -> m g u q e", g=PASSES, u=PAIR, e=PAIR),
                in_=pairs[1, s, tile // PAIR][:, tile % PAIR, :].rearrange(
                    "m (g q u e) -> m g u q e", g=PASSES, u=PAIR, e=PAIR
                ),
            )
            rounded[s, tile] = low

        def turn_hop(s, tile):
            words = rounded[s, tile][:].bitcast(F32)
            bank = banks.tile([P, PASSES, PAIR, P], F32, tag="bank")
            for g in range(PASSES):
                for u in range(PAIR):
                    start = (PAIR * g + u) * P
                    nc.tensor.transpose(bank[:, g, u, :], words[:, start : start + P], identity[:])
            held["hop", s, tile] = bank

        def copy_hop(s, tile, on_vector):
            if (s, tile // 2) not in hop_grouped:
                hop_grouped[s, tile // 2] = group_pool.tile(
                    [P, 2, PASSES, P, PACK], BF16, tag="grouped", align_bytes=64, name="grouped"
                )
            copy_out(
                on_vector,
                hop_grouped[s, tile // 2][:, tile % 2, :, :, :]
                .rearrange("p g c t -> p g (c t)")
                .bitcast(F32)
                .rearrange("p g (c u) -> p g c u", u=PAIR),
                held["hop", s, tile][:].rearrange("p g u c -> p g c u"),
            )

        def quantise_hop(s, first):
            nc.vector.quantize_mx(
                out=hop_mx[s][0][:, first : first + 2, :, :].rearrange("p a g m -> p (a g m)").bitcast(FP8X4),
                scales=hop_mx[s][1][:, first : first + 2, :, :].rearrange("p a g m -> p (a g m)"),
                in_=hop_grouped[s, first // 2][:].rearrange("p a g m t -> p (a g m t)"),
            )

        ctx.enter_context(tc.manual_schedule())

        def prepare_x(r, scalar_h):
            for g in range(PASSES):
                for h in range(2):
                    turn_x(r, h, g)
                    copy_x(r, h, g, SCALAR if h == scalar_h else VECTOR)

        def prepare_support(s, half, vector_banks):
            for jj in range(2):
                for g in range(PASSES):
                    turn_support(s, half, g, jj)
                    copy_support(s, half, g, jj, VECTOR if (jj, g) in vector_banks else SCALAR)

        def quantise_half(s, half):
            for g in range(PASSES):
                quantise_support(s, half, g)

        def first_result(s, tile, half, on_vector=SCALAR):
            copy_product(1, s, tile, half, on_vector)
            if half == HALVES - 1:
                store(1, s, tile, together=(s == 1))

        def first_hop(s, tile, vector_half=None):
            for half in range(HALVES):
                multiply(1, s, tile, half)
                first_result(s, tile, half, VECTOR if half == vector_half else SCALAR)

        prepare_x(0, scalar_h=0)
        quantise_x(0, 0)
        quantise_x(0, 1)
        prepare_support(0, 0, ())
        quantise_half(0, 0)
        prepare_support(0, 1, ((0, 1),))
        for g in range(PASSES):
            sort_x(g)
        quantise_half(0, 1)
        for tile in range(TILES):
            multiply(1, 0, tile, 0)
        for tile in range(TILES):
            first_result(0, tile, 0)
        for g in range(PASSES):
            for h in range(2):
                turn_sorted_x(h, g)
                copy_sorted_x(h, g, SCALAR if h == 1 else VECTOR)
        sort_words(1, 0, 0)
        sort_words(1, 0, 1)
        quantise_x(1, 0)
        for tile in range(TILES):
            multiply(1, 0, tile, 1)
            first_result(0, tile, 1)
        quantise_x(1, 1)
        sort_words(1, 1, 0)
        sort_words(1, 1, 1)
        prepare_support(1, 0, ((0, 0), (1, 0)))
        quantise_half(1, 0)
        first_hop(0, 4)
        first_hop(0, 5)
        prepare_support(1, 1, ((0, 0), (1, 0)))
        quantise_half(1, 1)
        first_hop(0, 6)
        first_hop(0, 7)

        def turn_tiles(s, r):
            tiles = range(TILES * r, TILES * (r + 1))
            for tile in tiles:
                turn_hop(s, tile)
                copy_hop(s, tile, VECTOR if tile % 2 == 0 else SCALAR)
            for first in tiles[::2]:
                quantise_hop(s, first)

        def second_hop(s, tile):
            for half in range(HALVES):
                multiply(2, s, tile, half)
                copy_product(2, s, tile, half, VECTOR if half == 0 else SCALAR)
            store(2, s, tile, together=False)

        for tile in range(TILES):
            round_hop(0, 2 * tile)
            round_hop(0, 2 * tile + 1)
            first_hop(1, tile)
        turn_tiles(0, 0)
        for tile in range(TILES):
            round_hop(1, tile)
            first_hop(1, TILES + tile)
        turn_tiles(0, 1)
        for tile in range(TILES):
            second_hop(0, tile)
            round_hop(1, TILES + tile)
        turn_tiles(1, 0)
        for tile in range(TILES, 2 * TILES):
            second_hop(0, tile)
        for tile in range(2):
            second_hop(1, tile)
        turn_tiles(1, 1)
        for tile in range(2, 2 * TILES):
            second_hop(1, tile)
